import numpy as np
import ml_dtypes


def mxq(x, axis, fmt="e4m3"):
    dtype, down = {"e4m3": (ml_dtypes.float8_e4m3fn, 7), "e5m2": (ml_dtypes.float8_e5m2, 14)}[fmt]
    v = np.moveaxis(np.asarray(x, np.float32).astype(ml_dtypes.bfloat16).astype(np.float64), axis, -1)
    blocks = v.reshape(v.shape[:-1] + (-1, 32))
    amax = np.abs(blocks).max(-1, keepdims=True)
    byte = np.maximum(np.where(amax > 0, np.frexp(amax)[1] - 1 + 127, 0) - down, 1)
    scale = np.exp2(byte - 127.0)
    codes = (blocks / scale).astype(np.float32).astype(dtype).astype(np.float64)
    return np.moveaxis((codes * scale).reshape(v.shape), -1, axis)


WIDE = False


def mx_kscale(k):
    if not WIDE:
        return np.ones(k)
    levels = np.array([10, -10, 5, -5, 0])
    a = np.random.permutation(np.resize(levels, k // 512 * 4)).reshape(k // 512, 4)
    idx = np.arange(k)
    return np.exp2(a[idx // 512, idx % 128 // 32])


BF16 = ml_dtypes.bfloat16


def bf(x):
    return np.asarray(x, np.float32).astype(BF16)


def f64(x):
    return np.asarray(x).astype(np.float64)


B, CIN, H, W = 2, 256, 32, 32
C = CIN + CIN
D = CIN
HW = H * W
QS = np.sqrt(2.0 / np.sqrt(D))
VS = 4.0


def setup_inputs():
    t = mx_kscale(C)
    return {"q": bf(np.random.standard_normal((B, HW, D)) * QS),
            "k": bf(np.random.standard_normal((B, D, HW)) * QS),
            "v": bf(np.random.standard_normal((B, C, HW)) * VS * t[:, None]),
            "x1": bf(np.random.standard_normal((B, CIN, H, W)) * t[:CIN, None, None]),
            "x2": bf(np.random.standard_normal((B, CIN, H, W)) * t[CIN:, None, None]),
            "Wsc": bf(np.random.standard_normal((D, C)) / np.sqrt(C) / t),
            "gamma": bf(0.5 + 0.1 * np.random.standard_normal(1))}


def reference(q, k, v, x1, x2, Wsc, gamma):
    x = np.concatenate([f64(x1), f64(x2)], axis=1).reshape(B, C, HW)
    am = f64(q) @ f64(k)
    e = np.exp(am - am.max(axis=1, keepdims=True))
    a = e / e.sum(axis=1, keepdims=True)
    agg = mxq(f64(v), 2, "e4m3") @ mxq(a, 2, "e4m3").transpose(0, 2, 1)
    y = f64(gamma)[0] * agg + x
    return (mxq(f64(Wsc), 1, "e4m3") @ mxq(y, 1, "e4m3")).reshape(B, D, H, W)

@@ -1,0 +1,355 @@
+from contextlib import ExitStack
+
+import concourse.mybir as mybir
+from concourse.masks import make_identity
+
+F32 = mybir.dt.float32
+BF16 = mybir.dt.bfloat16
+U32 = mybir.dt.uint32
+U8 = mybir.dt.uint8
+FP8X4 = mybir.dt.float8_e4m3fn_x4
+ALU = mybir.AluOpType
+ACT = mybir.ActivationFunctionType
+AXIS = mybir.AxisListType
+
+IMAGES = 2
+PIXELS = 1024
+D = 256
+C = 512
+
+P = 128
+PACK = 4
+K_PASS = P * PACK
+BANK = 512
+
+M_PASSES = PIXELS // K_PASS
+HALVES = PIXELS // BANK
+D_TILES = D // P
+C_TILES = C // P
+PIXEL_TILES = PIXELS // P
+ALL_KEY_TILES = IMAGES * PIXEL_TILES
+
+FLOPS = 2 * IMAGES * (PIXELS * PIXELS * D + C * PIXELS * PIXELS + D * C * PIXELS)
+
+
+def tile_featureaggregation_pa_kernel(tc, q, k, v, x1, x2, Wsc, gamma, out):
+    nc = tc.nc
+    with ExitStack() as ctx:
+        keep = ctx.enter_context(tc.tile_pool(name="keep", bufs=1))
+        small = ctx.enter_context(tc.tile_pool(name="small", bufs=4))
+        exp_pool = ctx.enter_context(tc.tile_pool(name="exp", bufs=3))
+        stage = ctx.enter_context(tc.tile_pool(name="stage", bufs=2))
+        result_pool = ctx.enter_context(tc.tile_pool(name="result", bufs=4))
+        psum_scores = ctx.enter_context(tc.psum_pool(name="psum_scores", bufs=4))
+        psum_agg = ctx.enter_context(tc.psum_pool(name="psum_agg", bufs=2))
+        psum_misc = ctx.enter_context(tc.psum_pool(name="psum_misc", bufs=2))
+
+        q_sb = [keep.tile([P, PIXEL_TILES, D], BF16, name="q_sb%d" % b) for b in range(IMAGES)]
+        k_sb = [keep.tile([P, D_TILES, PIXELS], BF16, name="k_sb%d" % b) for b in range(IMAGES)]
+        v_sb = [keep.tile([P, C_TILES, PIXELS], BF16, name="v_sb%d" % b) for b in range(IMAGES)]
+        x_sb = [keep.tile([P, C_TILES, PIXELS], BF16, name="x_sb%d" % b) for b in range(IMAGES)]
+        w_sb = keep.tile([P, D_TILES, C], BF16)
+        gain_bf = keep.tile([P, 1], BF16)
+
+        def load_q(b):
+            nc.sync.dma_start(out=q_sb[b][:], in_=q[b].rearrange("(i p) d -> p i d", p=P))
+
+        def load_k(b):
+            nc.sync.dma_start(out=k_sb[b][:], in_=k[b].rearrange("(i p) m -> p i m", p=P))
+
+        def load_v(b):
+            nc.sync.dma_start(out=v_sb[b][:], in_=v[b].rearrange("(i p) m -> p i m", p=P))
+
+        def load_x(b):
+            half = C_TILES // 2
+            nc.sync.dma_start(
+                out=x_sb[b][:, 0:half, :], in_=x1[b].rearrange("(i p) h w -> p i (h w)", p=P)
+            )
+            nc.sync.dma_start(
+                out=x_sb[b][:, half:C_TILES, :], in_=x2[b].rearrange("(i p) h w -> p i (h w)", p=P)
+            )
+
+        load_q(0)
+        load_k(0)
+        load_v(0)
+        nc.sync.dma_start(out=w_sb[:], in_=Wsc.rearrange("(i p) c -> p i c", p=P))
+        nc.sync.dma_start(out=gain_bf[:], in_=gamma.partition_broadcast(P))
+        load_q(1)
+        load_k(1)
+        load_v(1)
+        load_x(0)
+        load_x(1)
+
+        ident_bf = keep.tile([P, P], BF16)
+        make_identity(nc, ident_bf[:])
+        ident_f32 = keep.tile([P, P], F32)
+        make_identity(nc, ident_f32[:])
+        gain = keep.tile([P, 1], F32)
+        nc.vector.tensor_copy(out=gain[:], in_=gain_bf[:])
+
+        qT = [keep.tile([P, D_TILES, PIXELS], BF16, name="qT%d" % b) for b in range(IMAGES)]
+        v_codes = [
+            keep.tile([P, M_PASSES, C], U32, name="v_codes%d" % b, align_bytes=64)
+            for b in range(IMAGES)
+        ]
+        v_scales = [
+            keep.tile([P, M_PASSES, C], U8, name="v_scales%d" % b, align_bytes=64)
+            for b in range(IMAGES)
+        ]
+        a_codes = [
+            keep.tile([P, M_PASSES, PIXELS], U32, name="a_codes%d" % b, align_bytes=64)
+            for b in range(IMAGES)
+        ]
+        a_scales = [
+            keep.tile([P, M_PASSES, PIXELS], U8, name="a_scales%d" % b, align_bytes=64)
+            for b in range(IMAGES)
+        ]
+        y_grouped = [
+            keep.tile([P, PIXELS, PACK], BF16, name="y_grouped%d" % b, align_bytes=64)
+            for b in range(IMAGES)
+        ]
+        y_codes = [
+            keep.tile([P, PIXELS], U32, name="y_codes%d" % b, align_bytes=64)
+            for b in range(IMAGES)
+        ]
+        y_scales = [
+            keep.tile([P, PIXELS], U8, name="y_scales%d" % b, align_bytes=64)
+            for b in range(IMAGES)
+        ]
+        w_codes = keep.tile([P, D], U32, align_bytes=64)
+        w_scales = keep.tile([P, D], U8, align_bytes=64)
+
+        def prepare_q(b):
+            for i in range(D_TILES):
+                for h in range(HALVES):
+                    flipped = psum_misc.tile([P, BANK], BF16, tag="misc")
+                    for j in range(BANK // P):
+                        nc.tensor.transpose(
+                            flipped[:, j * P : (j + 1) * P],
+                            q_sb[b][:, h * (BANK // P) + j, i * P : (i + 1) * P],
+                            ident_bf[:],
+                        )
+                    nc.scalar.copy(out=qT[b][:, i, h * BANK : (h + 1) * BANK], in_=flipped[:])
+
+        def prepare_w():
+            w_grouped = stage.tile([P, D, PACK], BF16, align_bytes=64)
+            for i in range(D_TILES):
+                flipped = psum_misc.tile([P, PACK, P], BF16, tag="misc")
+                for t in range(PACK):
+                    nc.tensor.transpose(
+                        flipped[:, t, :], w_sb[:, i, t * P : (t + 1) * P], ident_bf[:]
+                    )
+                nc.vector.tensor_copy(
+                    out=w_grouped[:, i * P : (i + 1) * P, :],
+                    in_=flipped[:].rearrange("p t r -> p r t"),
+                )
+            nc.vector.quantize_mx(
+                out=w_codes[:].bitcast(FP8X4),
+                scales=w_scales[:],
+                in_=w_grouped[:].rearrange("p r t -> p (r t)"),
+            )
+
+        def prepare_v(b):
+            v_words = v_sb[b][:].bitcast(F32)
+            v_grouped = stage.tile([P, M_PASSES, C, PACK], BF16, align_bytes=64)
+            for g in range(M_PASSES):
+                for pair in range(C_TILES // 2):
+                    flipped = psum_misc.tile([P, 2, 2, P], F32, tag="misc")
+                    for i in range(2):
+                        for u in range(2):
+                            j = 2 * g + u
+                            nc.tensor.transpose(
+                                flipped[:, i, u, :],
+                                v_words[:, 2 * pair + i, j * P : (j + 1) * P],
+                                ident_f32[:],
+                            )
+                    nc.scalar.copy(
+                        out=v_grouped[:, g, 2 * pair * P : 2 * (pair + 1) * P, :]
+                        .bitcast(F32)
+                        .rearrange("p (i r) u -> p i r u", i=2),
+                        in_=flipped[:].rearrange("p i u r -> p i r u"),
+                    )
+            for g in range(M_PASSES):
+                nc.vector.quantize_mx(
+                    out=v_codes[b][:, g, :].bitcast(FP8X4),
+                    scales=v_scales[b][:, g, :],
+                    in_=v_grouped[:, g, :, :].rearrange("p r t -> p (r t)"),
+                )
+
+        def place(s):
+            b, rest = divmod(s, PIXEL_TILES)
+            g, t = divmod(rest, PACK)
+            return b, g, t
+
+        banks = {}
+        part_max = {}
+        neg_max = {}
+        exps = {}
+        part_sum = {}
+        total = {}
+        inverse = {}
+        a_rows = {}
+
+        def scores(s):
+            b, g, t = place(s)
+            u, e = divmod(t, 2)
+            banks[s] = []
+            for h in range(HALVES):
+                am = psum_scores.tile([P, BANK], F32)
+                for i in range(D_TILES):
+                    keys = k_sb[b][:, i, :].rearrange("p (j w e) -> p j e w", w=P, e=2)
+                    nc.tensor.matmul(
+                        out=am[:],
+                        lhsT=keys[:, 2 * g + u, e, :],
+                        rhs=qT[b][:, i, h * BANK : (h + 1) * BANK],
+                        start=(i == 0),
+                        stop=(i == D_TILES - 1),
+                    )
+                banks[s].append(am)
+
+        def bank_maxima(s):
+            part_max[s] = small.tile([P, HALVES], F32, name="part_max")
+            for h in range(HALVES):
+                nc.vector.tensor_reduce(
+                    out=part_max[s][:, h : h + 1], in_=banks[s][h][:], axis=AXIS.X, op=ALU.max
+                )
+
+        def negative_maximum(s):
+            neg_max[s] = small.tile([P, 1], F32, name="neg_max")
+            nc.vector.tensor_scalar(
+                out=neg_max[s][:],
+                in0=part_max[s][:, 0:1],
+                scalar1=part_max[s][:, 1:2],
+                scalar2=-1.0,
+                op0=ALU.max,
+                op1=ALU.mult,
+            )
+
+        def exponentials(s):
+            exps[s] = exp_pool.tile([P, PIXELS], F32, name="exps")
+            part_sum[s] = small.tile([P, HALVES], F32, name="part_sum")
+            for h in range(HALVES):
+                nc.scalar.activation(
+                    out=exps[s][:, h * BANK : (h + 1) * BANK],
+                    in_=banks[s][h][:],
+                    func=ACT.Exp,
+                    bias=neg_max[s][:, 0:1],
+                    scale=1.0,
+                    accum_out=part_sum[s][:, h : h + 1],
+                )
+
+        def column_sum(s):
+            total[s] = small.tile([P, 1], F32, name="total")
+            nc.vector.tensor_tensor(
+                out=total[s][:], in0=part_sum[s][:, 0:1], in1=part_sum[s][:, 1:2], op=ALU.add
+            )
+
+        def reciprocal_sum(s):
+            inverse[s] = small.tile([P, 1], F32, name="inverse")
+            nc.vector.reciprocal(out=inverse[s][:], in_=total[s][:])
+
+        def normalise(s):
+            b, g, t = place(s)
+            if t == 0:
+                a_rows[(b, g)] = stage.tile([P, PACK, PIXELS], BF16, name="a_rows")
+            nc.scalar.activation(
+                out=a_rows[(b, g)][:, t, :], in_=exps[s][:], func=ACT.Copy, scale=inverse[s][:, 0:1]
+            )
+
+        def quantise_a(b, g):
+            a_grouped = stage.tile([P, PIXELS, PACK], BF16, align_bytes=64)
+            for h in range(HALVES):
+                cols = slice(h * BANK, (h + 1) * BANK)
+                nc.vector.tensor_copy(
+                    out=a_grouped[:, cols, :].rearrange("p (c i) t -> p c t i", i=4),
+                    in_=a_rows[(b, g)][:, :, cols].rearrange("p t (c i) -> p c t i", i=4),
+                )
+            for h in range(HALVES):
+                cols = slice(h * BANK, (h + 1) * BANK)
+                nc.vector.quantize_mx(
+                    out=a_codes[b][:, g, cols].bitcast(FP8X4),
+                    scales=a_scales[b][:, g, cols],
+                    in_=a_grouped[:, cols, :].rearrange("p n t -> p (n t)"),
+                )
+
+        def aggregate(b, j):
+            cols = slice(j * P, (j + 1) * P)
+            agg = psum_agg.tile([P, C_TILES, P], F32)
+            for t in range(C_TILES):
+                rows = slice(t * P, (t + 1) * P)
+                for g in range(M_PASSES):
+                    nc.tensor.matmul_mx(
+                        out=agg[:, t, :],
+                        lhsT=v_codes[b][:, g, rows].bitcast(FP8X4),
+                        lhsT_scale=v_scales[b][:, g, rows],
+                        rhs=a_codes[b][:, g, cols].bitcast(FP8X4),
+                        rhs_scale=a_scales[b][:, g, cols],
+                        start=(g == 0),
+                        stop=(g == M_PASSES - 1),
+                    )
+            nc.vector.scalar_tensor_tensor(
+                out=y_grouped[b][:, cols, :],
+                in0=agg[:].rearrange("p t n -> p n t"),
+                scalar=gain[:, 0:1],
+                in1=x_sb[b][:, :, cols].rearrange("p t n -> p n t"),
+                op0=ALU.mult,
+                op1=ALU.add,
+            )
+
+        def project(b, h):
+            cols = slice(h * BANK, (h + 1) * BANK)
+            nc.vector.quantize_mx(
+                out=y_codes[b][:, cols].bitcast(FP8X4),
+                scales=y_scales[b][:, cols],
+                in_=y_grouped[b][:, cols, :].rearrange("p n t -> p (n t)"),
+            )
+            out_rows = out[b].rearrange("(i p) h w -> i p (h w)", p=P)
+            for i in range(D_TILES):
+                rows = slice(i * P, (i + 1) * P)
+                product = psum_misc.tile([P, BANK], F32, tag="misc")
+                nc.tensor.matmul_mx(
+                    out=product[:],
+                    lhsT=w_codes[:, rows].bitcast(FP8X4),
+                    lhsT_scale=w_scales[:, rows],
+                    rhs=y_codes[b][:, cols].bitcast(FP8X4),
+                    rhs_scale=y_scales[b][:, cols],
+                    start=True,
+                    stop=True,
+                )
+                result = result_pool.tile([P, BANK], F32)
+                nc.scalar.copy(out=result[:], in_=product[:])
+                nc.sync.dma_start(out=out_rows[i][:, cols], in_=result[:])
+
+        def finish(b, j):
+            aggregate(b, j)
+            if (j + 1) % (BANK // P) == 0:
+                project(b, j // (BANK // P))
+
+        prepare_q(0)
+        for s in range(ALL_KEY_TILES + 1):
+            if s < ALL_KEY_TILES:
+                scores(s)
+                bank_maxima(s)
+            if s >= 1:
+                column_sum(s - 1)
+            if s < ALL_KEY_TILES:
+                negative_maximum(s)
+            if s >= 1:
+                reciprocal_sum(s - 1)
+            if s < ALL_KEY_TILES:
+                exponentials(s)
+            if s >= 1:
+                normalise(s - 1)
+                b, g, t = place(s - 1)
+                if t == PACK - 1:
+                    quantise_a(b, g)
+            if s == 1:
+                prepare_v(0)
+                prepare_w()
+            if s == PIXEL_TILES // 2:
+                prepare_q(1)
+                prepare_v(1)
+            if s > PIXEL_TILES:
+                finish(0, s - PIXEL_TILES - 1)
+        for j in range(PIXEL_TILES):
+            finish(1, j)

@@ -28,6 +28,9 @@ D_TILES = D // P
 C_TILES = C // P
 PIXEL_TILES = PIXELS // P
 ALL_KEY_TILES = IMAGES * PIXEL_TILES
+OUT_COLS = BANK // D_TILES
+OUT_BLOCKS = PIXELS // OUT_COLS
+TILES_PER_BLOCK = OUT_COLS // P
 
 FLOPS = 2 * IMAGES * (PIXELS * PIXELS * D + C * PIXELS * PIXELS + D * C * PIXELS)
 
@@ -37,12 +40,12 @@ def tile_featureaggregation_pa_kernel(tc, q, k, v, x1, x2, Wsc, gamma, out):
     with ExitStack() as ctx:
         keep = ctx.enter_context(tc.tile_pool(name="keep", bufs=1))
         small = ctx.enter_context(tc.tile_pool(name="small", bufs=4))
-        exp_pool = ctx.enter_context(tc.tile_pool(name="exp", bufs=3))
+        exp_pool = ctx.enter_context(tc.tile_pool(name="exp", bufs=4))
         stage = ctx.enter_context(tc.tile_pool(name="stage", bufs=2))
         result_pool = ctx.enter_context(tc.tile_pool(name="result", bufs=4))
         psum_scores = ctx.enter_context(tc.psum_pool(name="psum_scores", bufs=4))
-        psum_agg = ctx.enter_context(tc.psum_pool(name="psum_agg", bufs=2))
-        psum_misc = ctx.enter_context(tc.psum_pool(name="psum_misc", bufs=2))
+        psum_side = ctx.enter_context(tc.psum_pool(name="psum_side", bufs=4))
+        ctx.enter_context(tc.manual_schedule())
 
         q_sb = [keep.tile([P, PIXEL_TILES, D], BF16, name="q_sb%d" % b) for b in range(IMAGES)]
         k_sb = [keep.tile([P, D_TILES, PIXELS], BF16, name="k_sb%d" % b) for b in range(IMAGES)]
@@ -51,11 +54,17 @@ def tile_featureaggregation_pa_kernel(tc, q, k, v, x1, x2, Wsc, gamma, out):
         w_sb = keep.tile([P, D_TILES, C], BF16)
         gain_bf = keep.tile([P, 1], BF16)
 
-        def load_q(b):
-            nc.sync.dma_start(out=q_sb[b][:], in_=q[b].rearrange("(i p) d -> p i d", p=P))
+        def load_q(b, h):
+            tiles = slice(h * (BANK // P), (h + 1) * (BANK // P))
+            nc.sync.dma_start(
+                out=q_sb[b][:, tiles, :], in_=q[b].rearrange("(i p) d -> p i d", p=P)[:, tiles, :]
+            )
 
-        def load_k(b):
-            nc.sync.dma_start(out=k_sb[b][:], in_=k[b].rearrange("(i p) m -> p i m", p=P))
+        def load_k(b, g):
+            cols = slice(g * K_PASS, (g + 1) * K_PASS)
+            nc.sync.dma_start(
+                out=k_sb[b][:, :, cols], in_=k[b].rearrange("(i p) m -> p i m", p=P)[:, :, cols]
+            )
 
         def load_v(b):
             nc.sync.dma_start(out=v_sb[b][:], in_=v[b].rearrange("(i p) m -> p i m", p=P))
@@ -69,13 +78,17 @@ def tile_featureaggregation_pa_kernel(tc, q, k, v, x1, x2, Wsc, gamma, out):
                 out=x_sb[b][:, half:C_TILES, :], in_=x2[b].rearrange("(i p) h w -> p i (h w)", p=P)
             )
 
-        load_q(0)
-        load_k(0)
+        load_q(0, 0)
+        load_k(0, 0)
+        load_q(0, 1)
+        load_k(0, 1)
         load_v(0)
         nc.sync.dma_start(out=w_sb[:], in_=Wsc.rearrange("(i p) c -> p i c", p=P))
         nc.sync.dma_start(out=gain_bf[:], in_=gamma.partition_broadcast(P))
-        load_q(1)
-        load_k(1)
+        load_q(1, 0)
+        load_q(1, 1)
+        load_k(1, 0)
+        load_k(1, 1)
         load_v(1)
         load_x(0)
         load_x(1)
@@ -85,7 +98,6 @@ def tile_featureaggregation_pa_kernel(tc, q, k, v, x1, x2, Wsc, gamma, out):
         ident_f32 = keep.tile([P, P], F32)
         make_identity(nc, ident_f32[:])
         gain = keep.tile([P, 1], F32)
-        nc.vector.tensor_copy(out=gain[:], in_=gain_bf[:])
 
         qT = [keep.tile([P, D_TILES, PIXELS], BF16, name="qT%d" % b) for b in range(IMAGES)]
         v_codes = [
@@ -116,65 +128,91 @@ def tile_featureaggregation_pa_kernel(tc, q, k, v, x1, x2, Wsc, gamma, out):
             keep.tile([P, PIXELS], U8, name="y_scales%d" % b, align_bytes=64)
             for b in range(IMAGES)
         ]
+        w_grouped = keep.tile([P, D, PACK], BF16, align_bytes=64)
         w_codes = keep.tile([P, D], U32, align_bytes=64)
         w_scales = keep.tile([P, D], U8, align_bytes=64)
 
-        def prepare_q(b):
-            for i in range(D_TILES):
-                for h in range(HALVES):
-                    flipped = psum_misc.tile([P, BANK], BF16, tag="misc")
-                    for j in range(BANK // P):
-                        nc.tensor.transpose(
-                            flipped[:, j * P : (j + 1) * P],
-                            q_sb[b][:, h * (BANK // P) + j, i * P : (i + 1) * P],
-                            ident_bf[:],
-                        )
-                    nc.scalar.copy(out=qT[b][:, i, h * BANK : (h + 1) * BANK], in_=flipped[:])
+        flipped = {}
+        v_grouped = {}
 
-        def prepare_w():
-            w_grouped = stage.tile([P, D, PACK], BF16, align_bytes=64)
+        def flip_q(b, h):
             for i in range(D_TILES):
-                flipped = psum_misc.tile([P, PACK, P], BF16, tag="misc")
-                for t in range(PACK):
+                bank = psum_side.tile([P, BANK], BF16, tag="side", name="q_bank")
+                for j in range(BANK // P):
                     nc.tensor.transpose(
-                        flipped[:, t, :], w_sb[:, i, t * P : (t + 1) * P], ident_bf[:]
+                        bank[:, j * P : (j + 1) * P],
+                        q_sb[b][:, h * (BANK // P) + j, i * P : (i + 1) * P],
+                        ident_bf[:],
                     )
-                nc.vector.tensor_copy(
-                    out=w_grouped[:, i * P : (i + 1) * P, :],
-                    in_=flipped[:].rearrange("p t r -> p r t"),
-                )
+                flipped[("q", b, h, i)] = bank
+
+        def unload_q(b, h):
+            cols = slice(h * BANK, (h + 1) * BANK)
+            nc.scalar.copy(out=qT[b][:, 0, cols], in_=flipped[("q", b, h, 0)][:])
+            nc.vector.tensor_copy(out=qT[b][:, 1, cols], in_=flipped[("q", b, h, 1)][:])
+
+        def flip_w():
+            for i in range(D_TILES):
+                bank = psum_side.tile([P, PACK, P], BF16, tag="side", name="w_bank")
+                for t in range(PACK):
+                    nc.tensor.transpose(bank[:, t, :], w_sb[:, i, t * P : (t + 1) * P], ident_bf[:])
+                flipped[("w", i)] = bank
+
+        def unload_w():
+            nc.scalar.copy(
+                out=w_grouped[:, 0:P, :], in_=flipped[("w", 0)][:].rearrange("p t r -> p r t")
+            )
+            nc.vector.tensor_copy(
+                out=w_grouped[:, P:D, :], in_=flipped[("w", 1)][:].rearrange("p t r -> p r t")
+            )
+
+        def pack_w():
             nc.vector.quantize_mx(
                 out=w_codes[:].bitcast(FP8X4),
                 scales=w_scales[:],
                 in_=w_grouped[:].rearrange("p r t -> p (r t)"),
             )
+            nc.vector.tensor_copy(out=gain[:], in_=gain_bf[:])
 
-        def prepare_v(b):
+        def flip_v(b, g):
             v_words = v_sb[b][:].bitcast(F32)
-            v_grouped = stage.tile([P, M_PASSES, C, PACK], BF16, align_bytes=64)
-            for g in range(M_PASSES):
-                for pair in range(C_TILES // 2):
-                    flipped = psum_misc.tile([P, 2, 2, P], F32, tag="misc")
-                    for i in range(2):
-                        for u in range(2):
-                            j = 2 * g + u
-                            nc.tensor.transpose(
-                                flipped[:, i, u, :],
-                                v_words[:, 2 * pair + i, j * P : (j + 1) * P],
-                                ident_f32[:],
-                            )
-                    nc.scalar.copy(
-                        out=v_grouped[:, g, 2 * pair * P : 2 * (pair + 1) * P, :]
-                        .bitcast(F32)
-                        .rearrange("p (i r) u -> p i r u", i=2),
-                        in_=flipped[:].rearrange("p i u r -> p i r u"),
-                    )
-            for g in range(M_PASSES):
-                nc.vector.quantize_mx(
-                    out=v_codes[b][:, g, :].bitcast(FP8X4),
-                    scales=v_scales[b][:, g, :],
-                    in_=v_grouped[:, g, :, :].rearrange("p r t -> p (r t)"),
-                )
+            for pair in range(C_TILES // 2):
+                bank = psum_side.tile([P, 2, 2, P], F32, tag="side", name="v_bank")
+                for i in range(2):
+                    for u in range(2):
+                        j = 2 * g + u
+                        nc.tensor.transpose(
+                            bank[:, i, u, :],
+                            v_words[:, 2 * pair + i, j * P : (j + 1) * P],
+                            ident_f32[:],
+                        )
+                flipped[("v", b, g, pair)] = bank
+
+        def unload_v(b, g):
+            v_grouped[(b, g)] = stage.tile([P, C, PACK], BF16, name="v_grouped", align_bytes=64)
+            words = v_grouped[(b, g)][:].bitcast(F32).rearrange("p (a i r) u -> p a i r u", a=2, i=2)
+            nc.scalar.copy(
+                out=words[:, 0], in_=flipped[("v", b, g, 0)][:].rearrange("p i u r -> p i r u")
+            )
+            nc.vector.tensor_copy(
+                out=words[:, 1], in_=flipped[("v", b, g, 1)][:].rearrange("p i u r -> p i r u")
+            )
+
+        def pack_v(b, g):
+            nc.vector.quantize_mx(
+                out=v_codes[b][:, g, :].bitcast(FP8X4),
+                scales=v_scales[b][:, g, :],
+                in_=v_grouped[(b, g)][:].rearrange("p r t -> p (r t)"),
+            )
+
+        def nothing():
+            return None
+
+        def job_v(b, g):
+            return (lambda: flip_v(b, g), lambda: unload_v(b, g), lambda: pack_v(b, g))
+
+        def job_q(b, h):
+            return (lambda: flip_q(b, h), lambda: unload_q(b, h), nothing)
 
         def place(s):
             b, rest = divmod(s, PIXEL_TILES)
@@ -189,6 +227,7 @@ def tile_featureaggregation_pa_kernel(tc, q, k, v, x1, x2, Wsc, gamma, out):
         total = {}
         inverse = {}
         a_rows = {}
+        a_grouped = {}
 
         def scores(s):
             b, g, t = place(s)
@@ -248,67 +287,103 @@ def tile_featureaggregation_pa_kernel(tc, q, k, v, x1, x2, Wsc, gamma, out):
             inverse[s] = small.tile([P, 1], F32, name="inverse")
             nc.vector.reciprocal(out=inverse[s][:], in_=total[s][:])
 
-        def normalise(s):
+        def a_row(s):
             b, g, t = place(s)
             if t == 0:
                 a_rows[(b, g)] = stage.tile([P, PACK, PIXELS], BF16, name="a_rows")
+            return a_rows[(b, g)][:, t, :]
+
+        def normalise(s):
             nc.scalar.activation(
-                out=a_rows[(b, g)][:, t, :], in_=exps[s][:], func=ACT.Copy, scale=inverse[s][:, 0:1]
+                out=a_row(s), in_=exps[s][:], func=ACT.Copy, scale=inverse[s][:, 0:1]
             )
 
-        def quantise_a(b, g):
-            a_grouped = stage.tile([P, PIXELS, PACK], BF16, align_bytes=64)
-            for h in range(HALVES):
-                cols = slice(h * BANK, (h + 1) * BANK)
-                nc.vector.tensor_copy(
-                    out=a_grouped[:, cols, :].rearrange("p (c i) t -> p c t i", i=4),
-                    in_=a_rows[(b, g)][:, :, cols].rearrange("p t (c i) -> p c t i", i=4),
-                )
-            for h in range(HALVES):
-                cols = slice(h * BANK, (h + 1) * BANK)
-                nc.vector.quantize_mx(
-                    out=a_codes[b][:, g, cols].bitcast(FP8X4),
-                    scales=a_scales[b][:, g, cols],
-                    in_=a_grouped[:, cols, :].rearrange("p n t -> p (n t)"),
-                )
-
-        def aggregate(b, j):
-            cols = slice(j * P, (j + 1) * P)
-            agg = psum_agg.tile([P, C_TILES, P], F32)
-            for t in range(C_TILES):
-                rows = slice(t * P, (t + 1) * P)
-                for g in range(M_PASSES):
-                    nc.tensor.matmul_mx(
-                        out=agg[:, t, :],
-                        lhsT=v_codes[b][:, g, rows].bitcast(FP8X4),
-                        lhsT_scale=v_scales[b][:, g, rows],
-                        rhs=a_codes[b][:, g, cols].bitcast(FP8X4),
-                        rhs_scale=a_scales[b][:, g, cols],
-                        start=(g == 0),
-                        stop=(g == M_PASSES - 1),
-                    )
-            nc.vector.scalar_tensor_tensor(
-                out=y_grouped[b][:, cols, :],
-                in0=agg[:].rearrange("p t n -> p n t"),
-                scalar=gain[:, 0:1],
-                in1=x_sb[b][:, :, cols].rearrange("p t n -> p n t"),
+        def normalise_on_both(s):
+            row = a_row(s)
+            nc.vector.tensor_scalar(
+                out=row[:, 0:BANK],
+                in0=exps[s][:, 0:BANK],
+                scalar1=inverse[s][:, 0:1],
+                scalar2=None,
                 op0=ALU.mult,
-                op1=ALU.add,
+            )
+            nc.scalar.activation(
+                out=row[:, BANK:PIXELS],
+                in_=exps[s][:, BANK:PIXELS],
+                func=ACT.Copy,
+                scale=inverse[s][:, 0:1],
             )
 
-        def project(b, h):
+        def regroup_a(b, g, h, copy):
+            if h == 0:
+                a_grouped[(b, g)] = stage.tile(
+                    [P, PIXELS, PACK], BF16, name="a_grouped", align_bytes=64
+                )
             cols = slice(h * BANK, (h + 1) * BANK)
+            copy(
+                out=a_grouped[(b, g)][:, cols, :].rearrange("p (c i) t -> p c t i", i=4),
+                in_=a_rows[(b, g)][:, :, cols].rearrange("p t (c i) -> p c t i", i=4),
+            )
+
+        def quantise_a(b, g, h):
+            cols = slice(h * BANK, (h + 1) * BANK)
+            nc.vector.quantize_mx(
+                out=a_codes[b][:, g, cols].bitcast(FP8X4),
+                scales=a_scales[b][:, g, cols],
+                in_=a_grouped[(b, g)][:, cols, :].rearrange("p n t -> p (n t)"),
+            )
+
+        agg_banks = {}
+        products = {}
+
+        def aggregate(b, r):
+            if not 0 <= r < OUT_BLOCKS:
+                return
+            for j in range(r * TILES_PER_BLOCK, (r + 1) * TILES_PER_BLOCK):
+                cols = slice(j * P, (j + 1) * P)
+                agg = psum_side.tile([P, C_TILES, P], F32, tag="side", name="agg")
+                for t in range(C_TILES):
+                    rows = slice(t * P, (t + 1) * P)
+                    for g in range(M_PASSES):
+                        nc.tensor.matmul_mx(
+                            out=agg[:, t, :],
+                            lhsT=v_codes[b][:, g, rows].bitcast(FP8X4),
+                            lhsT_scale=v_scales[b][:, g, rows],
+                            rhs=a_codes[b][:, g, cols].bitcast(FP8X4),
+                            rhs_scale=a_scales[b][:, g, cols],
+                            start=(g == 0),
+                            stop=(g == M_PASSES - 1),
+                        )
+                agg_banks[(b, j)] = agg
+
+        def residual(b, r):
+            if not 0 <= r < OUT_BLOCKS:
+                return
+            for j in range(r * TILES_PER_BLOCK, (r + 1) * TILES_PER_BLOCK):
+                cols = slice(j * P, (j + 1) * P)
+                nc.vector.scalar_tensor_tensor(
+                    out=y_grouped[b][:, cols, :],
+                    in0=agg_banks[(b, j)][:].rearrange("p t n -> p n t"),
+                    scalar=gain[:, 0:1],
+                    in1=x_sb[b][:, :, cols].rearrange("p t n -> p n t"),
+                    op0=ALU.mult,
+                    op1=ALU.add,
+                )
+
+        def project(b, r):
+            if not 0 <= r < OUT_BLOCKS:
+                return
+            cols = slice(r * OUT_COLS, (r + 1) * OUT_COLS)
             nc.vector.quantize_mx(
                 out=y_codes[b][:, cols].bitcast(FP8X4),
                 scales=y_scales[b][:, cols],
                 in_=y_grouped[b][:, cols, :].rearrange("p n t -> p (n t)"),
             )
-            out_rows = out[b].rearrange("(i p) h w -> i p (h w)", p=P)
+            product = psum_side.tile([P, D_TILES, OUT_COLS], F32, tag="side", name="product")
             for i in range(D_TILES):
                 rows = slice(i * P, (i + 1) * P)
-                product = psum_misc.tile([P, BANK], F32, tag="misc")
                 nc.tensor.matmul_mx(
-                    out=product[:],
+                    out=product[:, i, :],
                     lhsT=w_codes[:, rows].bitcast(FP8X4),
                     lhsT_scale=w_scales[:, rows],
                     rhs=y_codes[b][:, cols].bitcast(FP8X4),
@@ -316,40 +391,89 @@ def tile_featureaggregation_pa_kernel(tc, q, k, v, x1, x2, Wsc, gamma, out):
                     start=True,
                     stop=True,
                 )
-                result = result_pool.tile([P, BANK], F32)
-                nc.scalar.copy(out=result[:], in_=product[:])
-                nc.sync.dma_start(out=out_rows[i][:, cols], in_=result[:])
+            products[(b, r)] = product
 
-        def finish(b, j):
-            aggregate(b, j)
-            if (j + 1) % (BANK // P) == 0:
-                project(b, j // (BANK // P))
+        def store(b, r):
+            if not 0 <= r < OUT_BLOCKS:
+                return
+            cols = slice(r * OUT_COLS, (r + 1) * OUT_COLS)
+            result = result_pool.tile([P, D_TILES, OUT_COLS], F32)
+            nc.scalar.copy(out=result[:], in_=products[(b, r)][:])
+            nc.sync.dma_start(
+                out=out[b].rearrange("(i p) h w -> p i (h w)", p=P)[:, :, cols], in_=result[:]
+            )
 
-        prepare_q(0)
-        for s in range(ALL_KEY_TILES + 1):
-            if s < ALL_KEY_TILES:
-                scores(s)
-                bank_maxima(s)
-            if s >= 1:
-                column_sum(s - 1)
-            if s < ALL_KEY_TILES:
-                negative_maximum(s)
-            if s >= 1:
-                reciprocal_sum(s - 1)
-            if s < ALL_KEY_TILES:
-                exponentials(s)
+        jobs = [
+            job_v(0, 0),
+            job_v(0, 1),
+            (flip_w, unload_w, pack_w),
+            job_q(1, 0),
+            job_q(1, 1),
+            job_v(1, 0),
+            job_v(1, 1),
+        ]
+        REGROUP_LAG = 2
+        FINISH_STEP = PIXEL_TILES + REGROUP_LAG + 2
+
+        for h in range(HALVES):
+            flip_q(0, h)
+            unload_q(0, h)
+        scores(0)
+        bank_maxima(0)
+        negative_maximum(0)
+
+        for s in range(ALL_KEY_TILES):
+            r = s - FINISH_STEP
+            following = s + 1 < ALL_KEY_TILES
+            if following:
+                scores(s + 1)
+            if s < len(jobs):
+                jobs[s][0]()
+            aggregate(0, r)
+            exponentials(s)
             if s >= 1:
                 normalise(s - 1)
-                b, g, t = place(s - 1)
-                if t == PACK - 1:
-                    quantise_a(b, g)
-            if s == 1:
-                prepare_v(0)
-                prepare_w()
-            if s == PIXEL_TILES // 2:
-                prepare_q(1)
-                prepare_v(1)
-            if s > PIXEL_TILES:
-                finish(0, s - PIXEL_TILES - 1)
-        for j in range(PIXEL_TILES):
-            finish(1, j)
+            store(0, r - 3)
+            if 0 <= s - 1 < len(jobs):
+                jobs[s - 1][1]()
+            if 0 <= s - 2 < len(jobs):
+                jobs[s - 2][2]()
+            for lag in range(3):
+                b, g, t = place(max(s - REGROUP_LAG - lag, 0))
+                if s - REGROUP_LAG - lag >= 0 and t == PACK - 1:
+                    if lag < HALVES:
+                        regroup_a(b, g, lag, nc.vector.tensor_copy)
+                    else:
+                        quantise_a(b, g, 0)
+                        quantise_a(b, g, 1)
+            project(0, r - 2)
+            residual(0, r - 1)
+            if following:
+                bank_maxima(s + 1)
+            column_sum(s)
+            if following:
+                negative_maximum(s + 1)
+            reciprocal_sum(s)
+
+        last = ALL_KEY_TILES - 1
+        r = ALL_KEY_TILES - FINISH_STEP
+        normalise_on_both(last)
+        regroup_a(1, 1, 0, nc.vector.tensor_copy)
+        regroup_a(1, 1, 1, nc.scalar.copy)
+        aggregate(0, r)
+        store(0, r - 3)
+        project(0, r - 2)
+        residual(0, r - 1)
+        quantise_a(1, 1, 0)
+        aggregate(1, 0)
+        store(0, r - 2)
+        project(0, r - 1)
+        residual(0, r)
+        quantise_a(1, 1, 1)
+        for d in range(OUT_BLOCKS + 2):
+            aggregate(1, d + 1)
+            store(0, r - 1 + d)
+            project(0, r + d)
+            residual(1, d)
+            project(1, d - 1)
+            store(1, d - 2)

@@ -31,6 +31,7 @@ ALL_KEY_TILES = IMAGES * PIXEL_TILES
 OUT_COLS = BANK // D_TILES
 OUT_BLOCKS = PIXELS // OUT_COLS
 TILES_PER_BLOCK = OUT_COLS // P
+GPSIMD_COLS = 384
 
 FLOPS = 2 * IMAGES * (PIXELS * PIXELS * D + C * PIXELS * PIXELS + D * C * PIXELS)
 
@@ -294,8 +295,21 @@ def tile_featureaggregation_pa_kernel(tc, q, k, v, x1, x2, Wsc, gamma, out):
             return a_rows[(b, g)][:, t, :]
 
         def normalise(s):
+            row = a_row(s)
+            split = PIXELS - GPSIMD_COLS
             nc.scalar.activation(
-                out=a_row(s), in_=exps[s][:], func=ACT.Copy, scale=inverse[s][:, 0:1]
+                out=row[:, 0:split],
+                in_=exps[s][:, 0:split],
+                func=ACT.Copy,
+                scale=inverse[s][:, 0:1],
+            )
+            nc.gpsimd.tensor_scalar(
+                out=row[:, split:PIXELS],
+                in0=exps[s][:, split:PIXELS],
+                scalar1=inverse[s][:, 0:1],
+                scalar2=0.0,
+                op0=ALU.mult,
+                op1=ALU.add,
             )
 
         def normalise_on_both(s):
@@ -432,7 +446,7 @@ def tile_featureaggregation_pa_kernel(tc, q, k, v, x1, x2, Wsc, gamma, out):
             aggregate(0, r)
             exponentials(s)
             if s >= 1:
-                normalise(s - 1)
+                column_sum(s - 1)
             store(0, r - 3)
             if 0 <= s - 1 < len(jobs):
                 jobs[s - 1][1]()
@@ -448,15 +462,17 @@ def tile_featureaggregation_pa_kernel(tc, q, k, v, x1, x2, Wsc, gamma, out):
                         quantise_a(b, g, 1)
             project(0, r - 2)
             residual(0, r - 1)
+            if s >= 1:
+                reciprocal_sum(s - 1)
+                normalise(s - 1)
             if following:
                 bank_maxima(s + 1)
-            column_sum(s)
-            if following:
                 negative_maximum(s + 1)
-            reciprocal_sum(s)
 
         last = ALL_KEY_TILES - 1
         r = ALL_KEY_TILES - FINISH_STEP
+        column_sum(last)
+        reciprocal_sum(last)
         normalise_on_both(last)
         regroup_a(1, 1, 0, nc.vector.tensor_copy)
         regroup_a(1, 1, 1, nc.scalar.copy)

@@ -235,7 +235,7 @@ def tile_featureaggregation_pa_kernel(tc, q, k, v, x1, x2, Wsc, gamma, out):
             u, e = divmod(t, 2)
             banks[s] = []
             for h in range(HALVES):
-                am = psum_scores.tile([P, BANK], F32)
+                am = psum_scores.tile([P, BANK], F32, tag="scores")
                 for i in range(D_TILES):
                     keys = k_sb[b][:, i, :].rearrange("p (j w e) -> p j e w", w=P, e=2)
                     nc.tensor.matmul(
@@ -355,7 +355,10 @@ def tile_featureaggregation_pa_kernel(tc, q, k, v, x1, x2, Wsc, gamma, out):
                 return
             for j in range(r * TILES_PER_BLOCK, (r + 1) * TILES_PER_BLOCK):
                 cols = slice(j * P, (j + 1) * P)
-                agg = psum_side.tile([P, C_TILES, P], F32, tag="side", name="agg")
+                if b == 0:
+                    agg = psum_side.tile([P, C_TILES, P], F32, tag="side")
+                else:
+                    agg = psum_scores.tile([P, C_TILES, P], F32, tag="scores")
                 for t in range(C_TILES):
                     rows = slice(t * P, (t + 1) * P)
                     for g in range(M_PASSES):
@@ -427,7 +430,7 @@ def tile_featureaggregation_pa_kernel(tc, q, k, v, x1, x2, Wsc, gamma, out):
             job_v(1, 1),
         ]
         REGROUP_LAG = 2
-        FINISH_STEP = PIXEL_TILES + REGROUP_LAG + 2
+        FINISH_STEP = PIXEL_TILES + REGROUP_LAG + 3
 
         for h in range(HALVES):
             flip_q(0, h)
@@ -452,14 +455,6 @@ def tile_featureaggregation_pa_kernel(tc, q, k, v, x1, x2, Wsc, gamma, out):
                 jobs[s - 1][1]()
             if 0 <= s - 2 < len(jobs):
                 jobs[s - 2][2]()
-            for lag in range(3):
-                b, g, t = place(max(s - REGROUP_LAG - lag, 0))
-                if s - REGROUP_LAG - lag >= 0 and t == PACK - 1:
-                    if lag < HALVES:
-                        regroup_a(b, g, lag, nc.vector.tensor_copy)
-                    else:
-                        quantise_a(b, g, 0)
-                        quantise_a(b, g, 1)
             project(0, r - 2)
             residual(0, r - 1)
             if s >= 1:
@@ -468,6 +463,14 @@ def tile_featureaggregation_pa_kernel(tc, q, k, v, x1, x2, Wsc, gamma, out):
             if following:
                 bank_maxima(s + 1)
                 negative_maximum(s + 1)
+            for lag in range(3):
+                b, g, t = place(max(s - REGROUP_LAG - lag, 0))
+                if s - REGROUP_LAG - lag >= 0 and t == PACK - 1:
+                    if lag < HALVES:
+                        regroup_a(b, g, lag, nc.vector.tensor_copy)
+                    else:
+                        quantise_a(b, g, 0)
+                        quantise_a(b, g, 1)
 
         last = ALL_KEY_TILES - 1
         r = ALL_KEY_TILES - FINISH_STEP
@@ -476,19 +479,17 @@ def tile_featureaggregation_pa_kernel(tc, q, k, v, x1, x2, Wsc, gamma, out):
         normalise_on_both(last)
         regroup_a(1, 1, 0, nc.vector.tensor_copy)
         regroup_a(1, 1, 1, nc.scalar.copy)
-        aggregate(0, r)
-        store(0, r - 3)
-        project(0, r - 2)
-        residual(0, r - 1)
-        quantise_a(1, 1, 0)
-        aggregate(1, 0)
-        store(0, r - 2)
-        project(0, r - 1)
-        residual(0, r)
-        quantise_a(1, 1, 1)
+        for ahead in range(2):
+            aggregate(0, r + ahead)
+            store(0, r + ahead - 3)
+            project(0, r + ahead - 2)
+            residual(0, r + ahead - 1)
+            quantise_a(1, 1, ahead)
+            if ahead == 0:
+                aggregate(1, 0)
         for d in range(OUT_BLOCKS + 2):
             aggregate(1, d + 1)
-            store(0, r - 1 + d)
+            store(0, r + d - 1)
             project(0, r + d)
             residual(1, d)
             project(1, d - 1)

@@ -31,7 +31,8 @@ ALL_KEY_TILES = IMAGES * PIXEL_TILES
 OUT_COLS = BANK // D_TILES
 OUT_BLOCKS = PIXELS // OUT_COLS
 TILES_PER_BLOCK = OUT_COLS // P
-GPSIMD_COLS = 384
+GPSIMD_COLS = 256
+SPLIT = PIXELS - GPSIMD_COLS
 
 FLOPS = 2 * IMAGES * (PIXELS * PIXELS * D + C * PIXELS * PIXELS + D * C * PIXELS)
 
@@ -292,25 +293,31 @@ def tile_featureaggregation_pa_kernel(tc, q, k, v, x1, x2, Wsc, gamma, out):
             b, g, t = place(s)
             if t == 0:
                 a_rows[(b, g)] = stage.tile([P, PACK, PIXELS], BF16, name="a_rows")
+                a_grouped[(b, g)] = stage.tile(
+                    [P, PIXELS, PACK], BF16, name="a_grouped", align_bytes=64
+                )
             return a_rows[(b, g)][:, t, :]
 
-        def normalise(s):
-            row = a_row(s)
-            split = PIXELS - GPSIMD_COLS
-            nc.scalar.activation(
-                out=row[:, 0:split],
-                in_=exps[s][:, 0:split],
-                func=ACT.Copy,
-                scale=inverse[s][:, 0:1],
-            )
+        def normalise_on_gpsimd(s):
+            b, g, t = place(s)
             nc.gpsimd.tensor_scalar(
-                out=row[:, split:PIXELS],
-                in0=exps[s][:, split:PIXELS],
+                out=a_grouped[(b, g)][:, SPLIT:PIXELS, t],
+                in0=exps[s][:, SPLIT:PIXELS],
                 scalar1=inverse[s][:, 0:1],
                 scalar2=0.0,
                 op0=ALU.mult,
                 op1=ALU.add,
             )
+
+        def normalise(s):
+            row = a_row(s)
+            nc.scalar.activation(
+                out=row[:, 0:SPLIT],
+                in_=exps[s][:, 0:SPLIT],
+                func=ACT.Copy,
+                scale=inverse[s][:, 0:1],
+            )
+            normalise_on_gpsimd(s)
 
         def normalise_on_both(s):
             row = a_row(s)
@@ -322,18 +329,15 @@ def tile_featureaggregation_pa_kernel(tc, q, k, v, x1, x2, Wsc, gamma, out):
                 op0=ALU.mult,
             )
             nc.scalar.activation(
-                out=row[:, BANK:PIXELS],
-                in_=exps[s][:, BANK:PIXELS],
+                out=row[:, BANK:SPLIT],
+                in_=exps[s][:, BANK:SPLIT],
                 func=ACT.Copy,
                 scale=inverse[s][:, 0:1],
             )
+            normalise_on_gpsimd(s)
 
         def regroup_a(b, g, h, copy):
-            if h == 0:
-                a_grouped[(b, g)] = stage.tile(
-                    [P, PIXELS, PACK], BF16, name="a_grouped", align_bytes=64
-                )
-            cols = slice(h * BANK, (h + 1) * BANK)
+            cols = slice(h * BANK, min((h + 1) * BANK, SPLIT))
             copy(
                 out=a_grouped[(b, g)][:, cols, :].rearrange("p (c i) t -> p c t i", i=4),
                 in_=a_rows[(b, g)][:, :, cols].rearrange("p t (c i) -> p c t i", i=4),

@@ -452,20 +452,20 @@ def tile_featureaggregation_pa_kernel(tc, q, k, v, x1, x2, Wsc, gamma, out):
                 jobs[s][0]()
             aggregate(0, r)
             exponentials(s)
-            if s >= 1:
-                column_sum(s - 1)
             store(0, r - 3)
             if 0 <= s - 1 < len(jobs):
                 jobs[s - 1][1]()
-            if 0 <= s - 2 < len(jobs):
-                jobs[s - 2][2]()
-            project(0, r - 2)
             residual(0, r - 1)
             if s >= 1:
                 reciprocal_sum(s - 1)
                 normalise(s - 1)
             if following:
                 bank_maxima(s + 1)
+            column_sum(s)
+            if 0 <= s - 2 < len(jobs):
+                jobs[s - 2][2]()
+            project(0, r - 2)
+            if following:
                 negative_maximum(s + 1)
             for lag in range(3):
                 b, g, t = place(max(s - REGROUP_LAG - lag, 0))
@@ -478,19 +478,20 @@ def tile_featureaggregation_pa_kernel(tc, q, k, v, x1, x2, Wsc, gamma, out):
 
         last = ALL_KEY_TILES - 1
         r = ALL_KEY_TILES - FINISH_STEP
-        column_sum(last)
         reciprocal_sum(last)
+        aggregate(0, r)
+        store(0, r - 3)
+        project(0, r - 2)
         normalise_on_both(last)
+        residual(0, r - 1)
         regroup_a(1, 1, 0, nc.vector.tensor_copy)
         regroup_a(1, 1, 1, nc.scalar.copy)
-        for ahead in range(2):
-            aggregate(0, r + ahead)
-            store(0, r + ahead - 3)
-            project(0, r + ahead - 2)
-            residual(0, r + ahead - 1)
-            quantise_a(1, 1, ahead)
-            if ahead == 0:
-                aggregate(1, 0)
+        store(0, r - 2)
+        project(0, r - 1)
+        quantise_a(1, 1, 0)
+        aggregate(1, 0)
+        residual(0, r)
+        quantise_a(1, 1, 1)
         for d in range(OUT_BLOCKS + 2):
             aggregate(1, d + 1)
             store(0, r + d - 1)

@@ -1,4 +1,5 @@
 from contextlib import ExitStack
+from functools import partial
 
 import concourse.mybir as mybir
 from concourse.masks import make_identity
@@ -65,11 +66,14 @@ def tile_featureaggregation_pa_kernel(tc, q, k, v, x1, x2, Wsc, gamma, out):
         def load_k(b, g):
             cols = slice(g * K_PASS, (g + 1) * K_PASS)
             nc.sync.dma_start(
-                out=k_sb[b][:, :, cols], in_=k[b].rearrange("(i p) m -> p i m", p=P)[:, :, cols]
+                out=k_sb[b][:, :, cols], in_=k[b].rearrange("(p e) m -> p e m", e=2)[:, :, cols]
             )
 
-        def load_v(b):
-            nc.sync.dma_start(out=v_sb[b][:], in_=v[b].rearrange("(i p) m -> p i m", p=P))
+        def load_v(b, g):
+            cols = slice(g * K_PASS, (g + 1) * K_PASS)
+            nc.sync.dma_start(
+                out=v_sb[b][:, :, cols], in_=v[b].rearrange("(i p) m -> p i m", p=P)[:, :, cols]
+            )
 
         def load_x(b):
             half = C_TILES // 2
@@ -81,17 +85,19 @@ def tile_featureaggregation_pa_kernel(tc, q, k, v, x1, x2, Wsc, gamma, out):
             )
 
         load_q(0, 0)
-        load_k(0, 0)
         load_q(0, 1)
+        load_k(0, 0)
+        load_v(0, 0)
         load_k(0, 1)
-        load_v(0)
+        load_v(0, 1)
         nc.sync.dma_start(out=w_sb[:], in_=Wsc.rearrange("(i p) c -> p i c", p=P))
         nc.sync.dma_start(out=gain_bf[:], in_=gamma.partition_broadcast(P))
         load_q(1, 0)
         load_q(1, 1)
         load_k(1, 0)
         load_k(1, 1)
-        load_v(1)
+        load_v(1, 0)
+        load_v(1, 1)
         load_x(0)
         load_x(1)
 
@@ -101,7 +107,7 @@ def tile_featureaggregation_pa_kernel(tc, q, k, v, x1, x2, Wsc, gamma, out):
         make_identity(nc, ident_f32[:])
         gain = keep.tile([P, 1], F32)
 
-        qT = [keep.tile([P, D_TILES, PIXELS], BF16, name="qT%d" % b) for b in range(IMAGES)]
+        qT = [keep.tile([P, PIXELS, 2], BF16, name="qT%d" % b) for b in range(IMAGES)]
         v_codes = [
             keep.tile([P, M_PASSES, C], U32, name="v_codes%d" % b, align_bytes=64)
             for b in range(IMAGES)
@@ -134,24 +140,26 @@ def tile_featureaggregation_pa_kernel(tc, q, k, v, x1, x2, Wsc, gamma, out):
         w_codes = keep.tile([P, D], U32, align_bytes=64)
         w_scales = keep.tile([P, D], U8, align_bytes=64)
 
+        COPIES = (nc.scalar.copy, nc.vector.tensor_copy)
         flipped = {}
         v_grouped = {}
 
         def flip_q(b, h):
-            for i in range(D_TILES):
-                bank = psum_side.tile([P, BANK], BF16, tag="side", name="q_bank")
-                for j in range(BANK // P):
+            q_words = q_sb[b][:].bitcast(F32)
+            for i in range(2):
+                bank = psum_side.tile([P, BANK // 2], F32, tag="side", name="q_bank")
+                for j in range(BANK // 2 // P):
                     nc.tensor.transpose(
                         bank[:, j * P : (j + 1) * P],
-                        q_sb[b][:, h * (BANK // P) + j, i * P : (i + 1) * P],
-                        ident_bf[:],
+                        q_words[:, h * (BANK // P) + i * (BANK // 2 // P) + j, :],
+                        ident_f32[:],
                     )
                 flipped[("q", b, h, i)] = bank
 
-        def unload_q(b, h):
-            cols = slice(h * BANK, (h + 1) * BANK)
-            nc.scalar.copy(out=qT[b][:, 0, cols], in_=flipped[("q", b, h, 0)][:])
-            nc.vector.tensor_copy(out=qT[b][:, 1, cols], in_=flipped[("q", b, h, 1)][:])
+        def unload_q(b, h, i):
+            words = qT[b][:].rearrange("p n e -> p (n e)").bitcast(F32)
+            cols = slice(h * BANK + i * BANK // 2, h * BANK + (i + 1) * BANK // 2)
+            COPIES[i](out=words[:, cols], in_=flipped[("q", b, h, i)][:])
 
         def flip_w():
             for i in range(D_TILES):
@@ -160,12 +168,10 @@ def tile_featureaggregation_pa_kernel(tc, q, k, v, x1, x2, Wsc, gamma, out):
                     nc.tensor.transpose(bank[:, t, :], w_sb[:, i, t * P : (t + 1) * P], ident_bf[:])
                 flipped[("w", i)] = bank
 
-        def unload_w():
-            nc.scalar.copy(
-                out=w_grouped[:, 0:P, :], in_=flipped[("w", 0)][:].rearrange("p t r -> p r t")
-            )
-            nc.vector.tensor_copy(
-                out=w_grouped[:, P:D, :], in_=flipped[("w", 1)][:].rearrange("p t r -> p r t")
+        def unload_w(i):
+            COPIES[i](
+                out=w_grouped[:, i * P : (i + 1) * P, :],
+                in_=flipped[("w", i)][:].rearrange("p t r -> p r t"),
             )
 
         def pack_w():
@@ -176,9 +182,9 @@ def tile_featureaggregation_pa_kernel(tc, q, k, v, x1, x2, Wsc, gamma, out):
             )
             nc.vector.tensor_copy(out=gain[:], in_=gain_bf[:])
 
-        def flip_v(b, g):
+        def flip_v(b, g, pairs=(0, 1)):
             v_words = v_sb[b][:].bitcast(F32)
-            for pair in range(C_TILES // 2):
+            for pair in pairs:
                 bank = psum_side.tile([P, 2, 2, P], F32, tag="side", name="v_bank")
                 for i in range(2):
                     for u in range(2):
@@ -190,14 +196,12 @@ def tile_featureaggregation_pa_kernel(tc, q, k, v, x1, x2, Wsc, gamma, out):
                         )
                 flipped[("v", b, g, pair)] = bank
 
-        def unload_v(b, g):
-            v_grouped[(b, g)] = stage.tile([P, C, PACK], BF16, name="v_grouped", align_bytes=64)
+        def unload_v(b, g, i, copy=None):
+            if i == 0:
+                v_grouped[(b, g)] = stage.tile([P, C, PACK], BF16, name="v_grouped", align_bytes=64)
             words = v_grouped[(b, g)][:].bitcast(F32).rearrange("p (a i r) u -> p a i r u", a=2, i=2)
-            nc.scalar.copy(
-                out=words[:, 0], in_=flipped[("v", b, g, 0)][:].rearrange("p i u r -> p i r u")
-            )
-            nc.vector.tensor_copy(
-                out=words[:, 1], in_=flipped[("v", b, g, 1)][:].rearrange("p i u r -> p i r u")
+            (copy or COPIES[i])(
+                out=words[:, i], in_=flipped[("v", b, g, i)][:].rearrange("p i u r -> p i r u")
             )
 
         def pack_v(b, g):
@@ -211,10 +215,28 @@ def tile_featureaggregation_pa_kernel(tc, q, k, v, x1, x2, Wsc, gamma, out):
             return None
 
         def job_v(b, g):
-            return (lambda: flip_v(b, g), lambda: unload_v(b, g), lambda: pack_v(b, g))
+            return (
+                lambda: flip_v(b, g),
+                lambda: unload_v(b, g, 0),
+                lambda: unload_v(b, g, 1),
+                lambda: pack_v(b, g),
+            )
+
+        def half_job_v(b, g, i):
+            return (
+                lambda: flip_v(b, g, (i,)),
+                lambda: unload_v(b, g, i, nc.scalar.copy),
+                nothing,
+                (lambda: pack_v(b, g)) if i == 1 else nothing,
+            )
 
         def job_q(b, h):
-            return (lambda: flip_q(b, h), lambda: unload_q(b, h), nothing)
+            return (
+                lambda: flip_q(b, h),
+                lambda: unload_q(b, h, 0),
+                lambda: unload_q(b, h, 1),
+                nothing,
+            )
 
         def place(s):
             b, rest = divmod(s, PIXEL_TILES)
@@ -242,7 +264,7 @@ def tile_featureaggregation_pa_kernel(tc, q, k, v, x1, x2, Wsc, gamma, out):
                     nc.tensor.matmul(
                         out=am[:],
                         lhsT=keys[:, 2 * g + u, e, :],
-                        rhs=qT[b][:, i, h * BANK : (h + 1) * BANK],
+                        rhs=qT[b][:, h * BANK : (h + 1) * BANK, i],
                         start=(i == 0),
                         stop=(i == D_TILES - 1),
                     )
@@ -281,7 +303,7 @@ def tile_featureaggregation_pa_kernel(tc, q, k, v, x1, x2, Wsc, gamma, out):
 
         def column_sum(s):
             total[s] = small.tile([P, 1], F32, name="total")
-            nc.vector.tensor_tensor(
+            nc.gpsimd.tensor_tensor(
                 out=total[s][:], in0=part_sum[s][:, 0:1], in1=part_sum[s][:, 1:2], op=ALU.add
             )
 
@@ -311,33 +333,33 @@ def tile_featureaggregation_pa_kernel(tc, q, k, v, x1, x2, Wsc, gamma, out):
 
         def normalise(s):
             row = a_row(s)
+            mine = SPLIT if s < ALL_KEY_TILES - PACK else PIXELS
             nc.scalar.activation(
-                out=row[:, 0:SPLIT],
-                in_=exps[s][:, 0:SPLIT],
+                out=row[:, 0:mine],
+                in_=exps[s][:, 0:mine],
                 func=ACT.Copy,
                 scale=inverse[s][:, 0:1],
             )
-            normalise_on_gpsimd(s)
+            if mine < PIXELS:
+                normalise_on_gpsimd(s)
 
         def normalise_on_both(s):
             row = a_row(s)
             nc.vector.tensor_scalar(
-                out=row[:, 0:BANK],
-                in0=exps[s][:, 0:BANK],
+                out=row[:, 0:512],
+                in0=exps[s][:, 0:512],
                 scalar1=inverse[s][:, 0:1],
                 scalar2=None,
                 op0=ALU.mult,
             )
             nc.scalar.activation(
-                out=row[:, BANK:SPLIT],
-                in_=exps[s][:, BANK:SPLIT],
+                out=row[:, 512:PIXELS],
+                in_=exps[s][:, 512:PIXELS],
                 func=ACT.Copy,
                 scale=inverse[s][:, 0:1],
             )
-            normalise_on_gpsimd(s)
 
-        def regroup_a(b, g, h, copy):
-            cols = slice(h * BANK, min((h + 1) * BANK, SPLIT))
+        def regroup_a(b, g, cols, copy):
             copy(
                 out=a_grouped[(b, g)][:, cols, :].rearrange("p (c i) t -> p c t i", i=4),
                 in_=a_rows[(b, g)][:, :, cols].rearrange("p t (c i) -> p c t i", i=4),
@@ -381,15 +403,18 @@ def tile_featureaggregation_pa_kernel(tc, q, k, v, x1, x2, Wsc, gamma, out):
             if not 0 <= r < OUT_BLOCKS:
                 return
             for j in range(r * TILES_PER_BLOCK, (r + 1) * TILES_PER_BLOCK):
-                cols = slice(j * P, (j + 1) * P)
-                nc.vector.scalar_tensor_tensor(
-                    out=y_grouped[b][:, cols, :],
-                    in0=agg_banks[(b, j)][:].rearrange("p t n -> p n t"),
-                    scalar=gain[:, 0:1],
-                    in1=x_sb[b][:, :, cols].rearrange("p t n -> p n t"),
-                    op0=ALU.mult,
-                    op1=ALU.add,
-                )
+                residual_tile(b, j)
+
+        def residual_tile(b, j):
+            cols = slice(j * P, (j + 1) * P)
+            nc.vector.scalar_tensor_tensor(
+                out=y_grouped[b][:, cols, :],
+                in0=agg_banks[(b, j)][:].rearrange("p t n -> p n t"),
+                scalar=gain[:, 0:1],
+                in1=x_sb[b][:, :, cols].rearrange("p t n -> p n t"),
+                op0=ALU.mult,
+                op1=ALU.add,
+            )
 
         def project(b, r):
             if not 0 <= r < OUT_BLOCKS:
@@ -424,21 +449,24 @@ def tile_featureaggregation_pa_kernel(tc, q, k, v, x1, x2, Wsc, gamma, out):
                 out=out[b].rearrange("(i p) h w -> p i (h w)", p=P)[:, :, cols], in_=result[:]
             )
 
-        jobs = [
-            job_v(0, 0),
-            job_v(0, 1),
-            (flip_w, unload_w, pack_w),
-            job_q(1, 0),
-            job_q(1, 1),
-            job_v(1, 0),
-            job_v(1, 1),
-        ]
+        jobs = {
+            0: job_v(0, 0),
+            1: job_v(0, 1),
+            2: (flip_w, lambda: unload_w(0), lambda: unload_w(1), pack_w),
+            3: job_q(1, 0),
+            4: job_q(1, 1),
+            10: half_job_v(1, 0, 0),
+            11: half_job_v(1, 0, 1),
+            12: half_job_v(1, 1, 0),
+            13: half_job_v(1, 1, 1),
+        }
         REGROUP_LAG = 2
         FINISH_STEP = PIXEL_TILES + REGROUP_LAG + 3
 
         for h in range(HALVES):
             flip_q(0, h)
-            unload_q(0, h)
+            unload_q(0, h, 0)
+            unload_q(0, h, 1)
         scores(0)
         bank_maxima(0)
         negative_maximum(0)
@@ -448,33 +476,43 @@ def tile_featureaggregation_pa_kernel(tc, q, k, v, x1, x2, Wsc, gamma, out):
             following = s + 1 < ALL_KEY_TILES
             if following:
                 scores(s + 1)
-            if s < len(jobs):
+            if s in jobs:
                 jobs[s][0]()
             aggregate(0, r)
             exponentials(s)
+            column_sum(s)
             store(0, r - 3)
-            if 0 <= s - 1 < len(jobs):
+            bulk = []
+            if s - 1 in jobs:
                 jobs[s - 1][1]()
-            residual(0, r - 1)
+                bulk.append(jobs[s - 1][2])
+            if s - 2 in jobs:
+                bulk.append(jobs[s - 2][3])
+            if 0 <= r - 1 < OUT_BLOCKS:
+                bulk.append(partial(residual_tile, 0, 2 * r - 2))
+                bulk.append(partial(residual_tile, 0, 2 * r - 1))
+            if 0 <= r - 2 < OUT_BLOCKS:
+                bulk.append(partial(project, 0, r - 2))
+            for lag in range(3):
+                b, g, t = place(max(s - REGROUP_LAG - lag, 0))
+                if s - REGROUP_LAG - lag >= 0 and t == PACK - 1:
+                    if lag < HALVES:
+                        bulk.append(partial(regroup_a, b, g, slice(lag * BANK, min((lag + 1) * BANK, SPLIT)), nc.vector.tensor_copy))
+                    else:
+                        bulk.append(partial(quantise_a, b, g, 0))
+                        bulk.append(partial(quantise_a, b, g, 1))
+            bulk = [f for f in bulk if f != nothing]
             if s >= 1:
                 reciprocal_sum(s - 1)
                 normalise(s - 1)
             if following:
                 bank_maxima(s + 1)
-            column_sum(s)
-            if 0 <= s - 2 < len(jobs):
-                jobs[s - 2][2]()
-            project(0, r - 2)
+            for f in bulk[:1]:
+                f()
             if following:
                 negative_maximum(s + 1)
-            for lag in range(3):
-                b, g, t = place(max(s - REGROUP_LAG - lag, 0))
-                if s - REGROUP_LAG - lag >= 0 and t == PACK - 1:
-                    if lag < HALVES:
-                        regroup_a(b, g, lag, nc.vector.tensor_copy)
-                    else:
-                        quantise_a(b, g, 0)
-                        quantise_a(b, g, 1)
+            for f in bulk[1:]:
+                f()
 
         last = ALL_KEY_TILES - 1
         r = ALL_KEY_TILES - FINISH_STEP
@@ -484,8 +522,9 @@ def tile_featureaggregation_pa_kernel(tc, q, k, v, x1, x2, Wsc, gamma, out):
         project(0, r - 2)
         normalise_on_both(last)
         residual(0, r - 1)
-        regroup_a(1, 1, 0, nc.vector.tensor_copy)
-        regroup_a(1, 1, 1, nc.scalar.copy)
+        regroup_a(1, 1, slice(0, 256), nc.vector.tensor_copy)
+        regroup_a(1, 1, slice(256, 512), nc.vector.tensor_copy)
+        regroup_a(1, 1, slice(512, PIXELS), nc.scalar.copy)
         store(0, r - 2)
         project(0, r - 1)
         quantise_a(1, 1, 0)

@@ -45,7 +45,7 @@ def tile_featureaggregation_pa_kernel(tc, q, k, v, x1, x2, Wsc, gamma, out):
         small = ctx.enter_context(tc.tile_pool(name="small", bufs=4))
         exp_pool = ctx.enter_context(tc.tile_pool(name="exp", bufs=4))
         stage = ctx.enter_context(tc.tile_pool(name="stage", bufs=2))
-        result_pool = ctx.enter_context(tc.tile_pool(name="result", bufs=4))
+        result_pool = ctx.enter_context(tc.tile_pool(name="result", bufs=8))
         psum_scores = ctx.enter_context(tc.psum_pool(name="psum_scores", bufs=4))
         psum_side = ctx.enter_context(tc.psum_pool(name="psum_side", bufs=4))
         ctx.enter_context(tc.manual_schedule())
@@ -60,7 +60,8 @@ def tile_featureaggregation_pa_kernel(tc, q, k, v, x1, x2, Wsc, gamma, out):
         def load_q(b, h):
             tiles = slice(h * (BANK // P), (h + 1) * (BANK // P))
             nc.sync.dma_start(
-                out=q_sb[b][:, tiles, :], in_=q[b].rearrange("(i p) d -> p i d", p=P)[:, tiles, :]
+                out=q_sb[b][:, tiles, :].rearrange("p (i j) d -> p i j d", j=2),
+                in_=q[b].rearrange("(h i p j) d -> h p i j d", h=HALVES, i=2, j=2)[h],
             )
 
         def load_k(b, g):
@@ -159,7 +160,10 @@ def tile_featureaggregation_pa_kernel(tc, q, k, v, x1, x2, Wsc, gamma, out):
         def unload_q(b, h, i):
             words = qT[b][:].rearrange("p n e -> p (n e)").bitcast(F32)
             cols = slice(h * BANK + i * BANK // 2, h * BANK + (i + 1) * BANK // 2)
-            COPIES[i](out=words[:, cols], in_=flipped[("q", b, h, i)][:])
+            COPIES[i](
+                out=words[:, cols].rearrange("w (p j) -> w p j", j=2),
+                in_=flipped[("q", b, h, i)][:].rearrange("w (j p) -> w p j", j=2),
+            )
 
         def flip_w():
             for i in range(D_TILES):
@@ -416,16 +420,23 @@ def tile_featureaggregation_pa_kernel(tc, q, k, v, x1, x2, Wsc, gamma, out):
                 op1=ALU.add,
             )
 
-        def project(b, r):
-            if not 0 <= r < OUT_BLOCKS:
+        blocks = [(b, slice(n, n + OUT_COLS)) for b in range(IMAGES) for n in range(0, PIXELS, OUT_COLS)]
+        b, cols = blocks.pop()
+        middle = cols.start + OUT_COLS // 2
+        blocks += [(b, slice(cols.start, middle)), (b, slice(middle, cols.stop))]
+
+        def project(k):
+            if not 0 <= k < len(blocks):
                 return
-            cols = slice(r * OUT_COLS, (r + 1) * OUT_COLS)
+            b, cols = blocks[k]
             nc.vector.quantize_mx(
                 out=y_codes[b][:, cols].bitcast(FP8X4),
                 scales=y_scales[b][:, cols],
                 in_=y_grouped[b][:, cols, :].rearrange("p n t -> p (n t)"),
             )
-            product = psum_side.tile([P, D_TILES, OUT_COLS], F32, tag="side", name="product")
+            product = psum_side.tile(
+                [P, D_TILES, cols.stop - cols.start], F32, tag="side", name="product"
+            )
             for i in range(D_TILES):
                 rows = slice(i * P, (i + 1) * P)
                 nc.tensor.matmul_mx(
@@ -437,14 +448,14 @@ def tile_featureaggregation_pa_kernel(tc, q, k, v, x1, x2, Wsc, gamma, out):
                     start=True,
                     stop=True,
                 )
-            products[(b, r)] = product
+            products[k] = product
 
-        def store(b, r):
-            if not 0 <= r < OUT_BLOCKS:
+        def store(k):
+            if not 0 <= k < len(blocks):
                 return
-            cols = slice(r * OUT_COLS, (r + 1) * OUT_COLS)
-            result = result_pool.tile([P, D_TILES, OUT_COLS], F32)
-            nc.scalar.copy(out=result[:], in_=products[(b, r)][:])
+            b, cols = blocks[k]
+            result = result_pool.tile([P, D_TILES, cols.stop - cols.start], F32, name="result")
+            nc.scalar.copy(out=result[:], in_=products[k][:])
             nc.sync.dma_start(
                 out=out[b].rearrange("(i p) h w -> p i (h w)", p=P)[:, :, cols], in_=result[:]
             )
@@ -481,7 +492,7 @@ def tile_featureaggregation_pa_kernel(tc, q, k, v, x1, x2, Wsc, gamma, out):
             aggregate(0, r)
             exponentials(s)
             column_sum(s)
-            store(0, r - 3)
+            store(r - 3)
             bulk = []
             if s - 1 in jobs:
                 jobs[s - 1][1]()
@@ -492,7 +503,7 @@ def tile_featureaggregation_pa_kernel(tc, q, k, v, x1, x2, Wsc, gamma, out):
                 bulk.append(partial(residual_tile, 0, 2 * r - 2))
                 bulk.append(partial(residual_tile, 0, 2 * r - 1))
             if 0 <= r - 2 < OUT_BLOCKS:
-                bulk.append(partial(project, 0, r - 2))
+                bulk.append(partial(project, r - 2))
             for lag in range(3):
                 b, g, t = place(max(s - REGROUP_LAG - lag, 0))
                 if s - REGROUP_LAG - lag >= 0 and t == PACK - 1:
@@ -518,23 +529,31 @@ def tile_featureaggregation_pa_kernel(tc, q, k, v, x1, x2, Wsc, gamma, out):
         r = ALL_KEY_TILES - FINISH_STEP
         reciprocal_sum(last)
         aggregate(0, r)
-        store(0, r - 3)
-        project(0, r - 2)
+        store(r - 3)
+        project(r - 2)
         normalise_on_both(last)
         residual(0, r - 1)
         regroup_a(1, 1, slice(0, 256), nc.vector.tensor_copy)
         regroup_a(1, 1, slice(256, 512), nc.vector.tensor_copy)
         regroup_a(1, 1, slice(512, PIXELS), nc.scalar.copy)
-        store(0, r - 2)
-        project(0, r - 1)
+        store(r - 2)
+        project(r - 1)
         quantise_a(1, 1, 0)
         aggregate(1, 0)
         residual(0, r)
         quantise_a(1, 1, 1)
-        for d in range(OUT_BLOCKS + 2):
+        for d in range(OUT_BLOCKS):
             aggregate(1, d + 1)
-            store(0, r + d - 1)
-            project(0, r + d)
-            residual(1, d)
-            project(1, d - 1)
-            store(1, d - 2)
+            store(r - 1 + d)
+            if d == 0:
+                project(r)
+            residual_tile(1, 2 * d)
+            if d == OUT_BLOCKS - 1:
+                project(r + d)
+            residual_tile(1, 2 * d + 1)
+            if 0 < d < OUT_BLOCKS - 1:
+                project(r + d)
+        for k in range(r - 1 + OUT_BLOCKS, len(blocks)):
+            if k < len(blocks) - 1:
+                project(k + 1)
+            store(k)

@@ -513,11 +513,11 @@ def tile_featureaggregation_pa_kernel(tc, q, k, v, x1, x2, Wsc, gamma, out):
                         bulk.append(partial(quantise_a, b, g, 0))
                         bulk.append(partial(quantise_a, b, g, 1))
             bulk = [f for f in bulk if f != nothing]
+            if following:
+                bank_maxima(s + 1)
             if s >= 1:
                 reciprocal_sum(s - 1)
                 normalise(s - 1)
-            if following:
-                bank_maxima(s + 1)
             for f in bulk[:1]:
                 f()
             if following:

@@ -32,7 +32,7 @@ ALL_KEY_TILES = IMAGES * PIXEL_TILES
 OUT_COLS = BANK // D_TILES
 OUT_BLOCKS = PIXELS // OUT_COLS
 TILES_PER_BLOCK = OUT_COLS // P
-GPSIMD_COLS = 256
+GPSIMD_COLS = 288
 SPLIT = PIXELS - GPSIMD_COLS
 
 FLOPS = 2 * IMAGES * (PIXELS * PIXELS * D + C * PIXELS * PIXELS + D * C * PIXELS)
@@ -102,10 +102,17 @@ def tile_featureaggregation_pa_kernel(tc, q, k, v, x1, x2, Wsc, gamma, out):
         load_x(0)
         load_x(1)
 
-        ident_bf = keep.tile([P, P], BF16)
-        make_identity(nc, ident_bf[:])
+        zeros = keep.tile([P, 2 * P], BF16)
+        nc.vector.memset(zeros[:], 0.0)
+        for i in range(4):
+            idle = psum_scores.tile([P, 2 * P], F32, tag="scores", name="idle")
+            nc.tensor.matmul(out=idle[:], lhsT=zeros[:, 0:P], rhs=zeros[:], start=True, stop=True)
+
         ident_f32 = keep.tile([P, P], F32)
-        make_identity(nc, ident_f32[:])
+        nc.vector.memset(ident_f32[:], 0.0)
+        make_identity(nc, ident_f32[:], nomemset=True)
+        ident_bf = keep.tile([P, P], BF16)
+        nc.vector.tensor_copy(out=ident_bf[:], in_=ident_f32[:])
         gain = keep.tile([P, 1], F32)
 
         qT = [keep.tile([P, PIXELS, 2], BF16, name="qT%d" % b) for b in range(IMAGES)]

from contextlib import ExitStack
from functools import partial

import concourse.mybir as mybir
from concourse.masks import make_identity

F32 = mybir.dt.float32
BF16 = mybir.dt.bfloat16
U32 = mybir.dt.uint32
U8 = mybir.dt.uint8
FP8X4 = mybir.dt.float8_e4m3fn_x4
ALU = mybir.AluOpType
ACT = mybir.ActivationFunctionType
AXIS = mybir.AxisListType

IMAGES = 2
PIXELS = 1024
D = 256
C = 512

P = 128
PACK = 4
K_PASS = P * PACK
BANK = 512

M_PASSES = PIXELS // K_PASS
HALVES = PIXELS // BANK
D_TILES = D // P
C_TILES = C // P
PIXEL_TILES = PIXELS // P
ALL_KEY_TILES = IMAGES * PIXEL_TILES
OUT_COLS = BANK // D_TILES
OUT_BLOCKS = PIXELS // OUT_COLS
TILES_PER_BLOCK = OUT_COLS // P
GPSIMD_COLS = 288
SPLIT = PIXELS - GPSIMD_COLS

FLOPS = 2 * IMAGES * (PIXELS * PIXELS * D + C * PIXELS * PIXELS + D * C * PIXELS)


def tile_featureaggregation_pa_kernel(tc, q, k, v, x1, x2, Wsc, gamma, out):
    nc = tc.nc
    with ExitStack() as ctx:
        keep = ctx.enter_context(tc.tile_pool(name="keep", bufs=1))
        small = ctx.enter_context(tc.tile_pool(name="small", bufs=4))
        exp_pool = ctx.enter_context(tc.tile_pool(name="exp", bufs=4))
        stage = ctx.enter_context(tc.tile_pool(name="stage", bufs=2))
        result_pool = ctx.enter_context(tc.tile_pool(name="result", bufs=8))
        psum_scores = ctx.enter_context(tc.psum_pool(name="psum_scores", bufs=4))
        psum_side = ctx.enter_context(tc.psum_pool(name="psum_side", bufs=4))
        ctx.enter_context(tc.manual_schedule())

        q_sb = [keep.tile([P, PIXEL_TILES, D], BF16, name="q_sb%d" % b) for b in range(IMAGES)]
        k_sb = [keep.tile([P, D_TILES, PIXELS], BF16, name="k_sb%d" % b) for b in range(IMAGES)]
        v_sb = [keep.tile([P, C_TILES, PIXELS], BF16, name="v_sb%d" % b) for b in range(IMAGES)]
        x_sb = [keep.tile([P, C_TILES, PIXELS], BF16, name="x_sb%d" % b) for b in range(IMAGES)]
        w_sb = keep.tile([P, D_TILES, C], BF16)
        gain_bf = keep.tile([P, 1], BF16)

        def load_q(b, h):
            tiles = slice(h * (BANK // P), (h + 1) * (BANK // P))
            nc.sync.dma_start(
                out=q_sb[b][:, tiles, :].rearrange("p (i j) d -> p i j d", j=2),
                in_=q[b].rearrange("(h i p j) d -> h p i j d", h=HALVES, i=2, j=2)[h],
            )

        def load_k(b, g):
            cols = slice(g * K_PASS, (g + 1) * K_PASS)
            nc.sync.dma_start(
                out=k_sb[b][:, :, cols], in_=k[b].rearrange("(p e) m -> p e m", e=2)[:, :, cols]
            )

        def load_v(b, g):
            cols = slice(g * K_PASS, (g + 1) * K_PASS)
            nc.sync.dma_start(
                out=v_sb[b][:, :, cols], in_=v[b].rearrange("(i p) m -> p i m", p=P)[:, :, cols]
            )

        def load_x(b):
            half = C_TILES // 2
            nc.sync.dma_start(
                out=x_sb[b][:, 0:half, :], in_=x1[b].rearrange("(i p) h w -> p i (h w)", p=P)
            )
            nc.sync.dma_start(
                out=x_sb[b][:, half:C_TILES, :], in_=x2[b].rearrange("(i p) h w -> p i (h w)", p=P)
            )

        load_q(0, 0)
        load_q(0, 1)
        load_k(0, 0)
        load_v(0, 0)
        load_k(0, 1)
        load_v(0, 1)
        nc.sync.dma_start(out=w_sb[:], in_=Wsc.rearrange("(i p) c -> p i c", p=P))
        nc.sync.dma_start(out=gain_bf[:], in_=gamma.partition_broadcast(P))
        load_q(1, 0)
        load_q(1, 1)
        load_k(1, 0)
        load_k(1, 1)
        load_v(1, 0)
        load_v(1, 1)
        load_x(0)
        load_x(1)

        zeros = keep.tile([P, 2 * P], BF16)
        nc.vector.memset(zeros[:], 0.0)
        for i in range(4):
            idle = psum_scores.tile([P, 2 * P], F32, tag="scores", name="idle")
            nc.tensor.matmul(out=idle[:], lhsT=zeros[:, 0:P], rhs=zeros[:], start=True, stop=True)

        ident_f32 = keep.tile([P, P], F32)
        nc.vector.memset(ident_f32[:], 0.0)
        make_identity(nc, ident_f32[:], nomemset=True)
        ident_bf = keep.tile([P, P], BF16)
        nc.vector.tensor_copy(out=ident_bf[:], in_=ident_f32[:])
        gain = keep.tile([P, 1], F32)

        qT = [keep.tile([P, PIXELS, 2], BF16, name="qT%d" % b) for b in range(IMAGES)]
        v_codes = [
            keep.tile([P, M_PASSES, C], U32, name="v_codes%d" % b, align_bytes=64)
            for b in range(IMAGES)
        ]
        v_scales = [
            keep.tile([P, M_PASSES, C], U8, name="v_scales%d" % b, align_bytes=64)
            for b in range(IMAGES)
        ]
        a_codes = [
            keep.tile([P, M_PASSES, PIXELS], U32, name="a_codes%d" % b, align_bytes=64)
            for b in range(IMAGES)
        ]
        a_scales = [
            keep.tile([P, M_PASSES, PIXELS], U8, name="a_scales%d" % b, align_bytes=64)
            for b in range(IMAGES)
        ]
        y_grouped = [
            keep.tile([P, PIXELS, PACK], BF16, name="y_grouped%d" % b, align_bytes=64)
            for b in range(IMAGES)
        ]
        y_codes = [
            keep.tile([P, PIXELS], U32, name="y_codes%d" % b, align_bytes=64)
            for b in range(IMAGES)
        ]
        y_scales = [
            keep.tile([P, PIXELS], U8, name="y_scales%d" % b, align_bytes=64)
            for b in range(IMAGES)
        ]
        w_grouped = keep.tile([P, D, PACK], BF16, align_bytes=64)
        w_codes = keep.tile([P, D], U32, align_bytes=64)
        w_scales = keep.tile([P, D], U8, align_bytes=64)

        COPIES = (nc.scalar.copy, nc.vector.tensor_copy)
        flipped = {}
        v_grouped = {}

        def flip_q(b, h):
            q_words = q_sb[b][:].bitcast(F32)
            for i in range(2):
                bank = psum_side.tile([P, BANK // 2], F32, tag="side", name="q_bank")
                for j in range(BANK // 2 // P):
                    nc.tensor.transpose(
                        bank[:, j * P : (j + 1) * P],
                        q_words[:, h * (BANK // P) + i * (BANK // 2 // P) + j, :],
                        ident_f32[:],
                    )
                flipped[("q", b, h, i)] = bank

        def unload_q(b, h, i):
            words = qT[b][:].rearrange("p n e -> p (n e)").bitcast(F32)
            cols = slice(h * BANK + i * BANK // 2, h * BANK + (i + 1) * BANK // 2)
            COPIES[i](
                out=words[:, cols].rearrange("w (p j) -> w p j", j=2),
                in_=flipped[("q", b, h, i)][:].rearrange("w (j p) -> w p j", j=2),
            )

        def flip_w():
            for i in range(D_TILES):
                bank = psum_side.tile([P, PACK, P], BF16, tag="side", name="w_bank")
                for t in range(PACK):
                    nc.tensor.transpose(bank[:, t, :], w_sb[:, i, t * P : (t + 1) * P], ident_bf[:])
                flipped[("w", i)] = bank

        def unload_w(i):
            COPIES[i](
                out=w_grouped[:, i * P : (i + 1) * P, :],
                in_=flipped[("w", i)][:].rearrange("p t r -> p r t"),
            )

        def pack_w():
            nc.vector.quantize_mx(
                out=w_codes[:].bitcast(FP8X4),
                scales=w_scales[:],
                in_=w_grouped[:].rearrange("p r t -> p (r t)"),
            )
            nc.vector.tensor_copy(out=gain[:], in_=gain_bf[:])

        def flip_v(b, g, pairs=(0, 1)):
            v_words = v_sb[b][:].bitcast(F32)
            for pair in pairs:
                bank = psum_side.tile([P, 2, 2, P], F32, tag="side", name="v_bank")
                for i in range(2):
                    for u in range(2):
                        j = 2 * g + u
                        nc.tensor.transpose(
                            bank[:, i, u, :],
                            v_words[:, 2 * pair + i, j * P : (j + 1) * P],
                            ident_f32[:],
                        )
                flipped[("v", b, g, pair)] = bank

        def unload_v(b, g, i, copy=None):
            if i == 0:
                v_grouped[(b, g)] = stage.tile([P, C, PACK], BF16, name="v_grouped", align_bytes=64)
            words = v_grouped[(b, g)][:].bitcast(F32).rearrange("p (a i r) u -> p a i r u", a=2, i=2)
            (copy or COPIES[i])(
                out=words[:, i], in_=flipped[("v", b, g, i)][:].rearrange("p i u r -> p i r u")
            )

        def pack_v(b, g):
            nc.vector.quantize_mx(
                out=v_codes[b][:, g, :].bitcast(FP8X4),
                scales=v_scales[b][:, g, :],
                in_=v_grouped[(b, g)][:].rearrange("p r t -> p (r t)"),
            )

        def nothing():
            return None

        def job_v(b, g):
            return (
                lambda: flip_v(b, g),
                lambda: unload_v(b, g, 0),
                lambda: unload_v(b, g, 1),
                lambda: pack_v(b, g),
            )

        def half_job_v(b, g, i):
            return (
                lambda: flip_v(b, g, (i,)),
                lambda: unload_v(b, g, i, nc.scalar.copy),
                nothing,
                (lambda: pack_v(b, g)) if i == 1 else nothing,
            )

        def job_q(b, h):
            return (
                lambda: flip_q(b, h),
                lambda: unload_q(b, h, 0),
                lambda: unload_q(b, h, 1),
                nothing,
            )

        def place(s):
            b, rest = divmod(s, PIXEL_TILES)
            g, t = divmod(rest, PACK)
            return b, g, t

        banks = {}
        part_max = {}
        neg_max = {}
        exps = {}
        part_sum = {}
        total = {}
        inverse = {}
        a_rows = {}
        a_grouped = {}

        def scores(s):
            b, g, t = place(s)
            u, e = divmod(t, 2)
            banks[s] = []
            for h in range(HALVES):
                am = psum_scores.tile([P, BANK], F32, tag="scores")
                for i in range(D_TILES):
                    keys = k_sb[b][:, i, :].rearrange("p (j w e) -> p j e w", w=P, e=2)
                    nc.tensor.matmul(
                        out=am[:],
                        lhsT=keys[:, 2 * g + u, e, :],
                        rhs=qT[b][:, h * BANK : (h + 1) * BANK, i],
                        start=(i == 0),
                        stop=(i == D_TILES - 1),
                    )
                banks[s].append(am)

        def bank_maxima(s):
            part_max[s] = small.tile([P, HALVES], F32, name="part_max")
            for h in range(HALVES):
                nc.vector.tensor_reduce(
                    out=part_max[s][:, h : h + 1], in_=banks[s][h][:], axis=AXIS.X, op=ALU.max
                )

        def negative_maximum(s):
            neg_max[s] = small.tile([P, 1], F32, name="neg_max")
            nc.vector.tensor_scalar(
                out=neg_max[s][:],
                in0=part_max[s][:, 0:1],
                scalar1=part_max[s][:, 1:2],
                scalar2=-1.0,
                op0=ALU.max,
                op1=ALU.mult,
            )

        def exponentials(s):
            exps[s] = exp_pool.tile([P, PIXELS], F32, name="exps")
            part_sum[s] = small.tile([P, HALVES], F32, name="part_sum")
            for h in range(HALVES):
                nc.scalar.activation(
                    out=exps[s][:, h * BANK : (h + 1) * BANK],
                    in_=banks[s][h][:],
                    func=ACT.Exp,
                    bias=neg_max[s][:, 0:1],
                    scale=1.0,
                    accum_out=part_sum[s][:, h : h + 1],
                )

        def column_sum(s):
            total[s] = small.tile([P, 1], F32, name="total")
            nc.gpsimd.tensor_tensor(
                out=total[s][:], in0=part_sum[s][:, 0:1], in1=part_sum[s][:, 1:2], op=ALU.add
            )

        def reciprocal_sum(s):
            inverse[s] = small.tile([P, 1], F32, name="inverse")
            nc.vector.reciprocal(out=inverse[s][:], in_=total[s][:])

        def a_row(s):
            b, g, t = place(s)
            if t == 0:
                a_rows[(b, g)] = stage.tile([P, PACK, PIXELS], BF16, name="a_rows")
                a_grouped[(b, g)] = stage.tile(
                    [P, PIXELS, PACK], BF16, name="a_grouped", align_bytes=64
                )
            return a_rows[(b, g)][:, t, :]

        def normalise_on_gpsimd(s):
            b, g, t = place(s)
            nc.gpsimd.tensor_scalar(
                out=a_grouped[(b, g)][:, SPLIT:PIXELS, t],
                in0=exps[s][:, SPLIT:PIXELS],
                scalar1=inverse[s][:, 0:1],
                scalar2=0.0,
                op0=ALU.mult,
                op1=ALU.add,
            )

        def normalise(s):
            row = a_row(s)
            mine = SPLIT if s < ALL_KEY_TILES - PACK else PIXELS
            nc.scalar.activation(
                out=row[:, 0:mine],
                in_=exps[s][:, 0:mine],
                func=ACT.Copy,
                scale=inverse[s][:, 0:1],
            )
            if mine < PIXELS:
                normalise_on_gpsimd(s)

        def normalise_on_both(s):
            row = a_row(s)
            nc.vector.tensor_scalar(
                out=row[:, 0:512],
                in0=exps[s][:, 0:512],
                scalar1=inverse[s][:, 0:1],
                scalar2=None,
                op0=ALU.mult,
            )
            nc.scalar.activation(
                out=row[:, 512:PIXELS],
                in_=exps[s][:, 512:PIXELS],
                func=ACT.Copy,
                scale=inverse[s][:, 0:1],
            )

        def regroup_a(b, g, cols, copy):
            copy(
                out=a_grouped[(b, g)][:, cols, :].rearrange("p (c i) t -> p c t i", i=4),
                in_=a_rows[(b, g)][:, :, cols].rearrange("p t (c i) -> p c t i", i=4),
            )

        def quantise_a(b, g, h):
            cols = slice(h * BANK, (h + 1) * BANK)
            nc.vector.quantize_mx(
                out=a_codes[b][:, g, cols].bitcast(FP8X4),
                scales=a_scales[b][:, g, cols],
                in_=a_grouped[(b, g)][:, cols, :].rearrange("p n t -> p (n t)"),
            )

        agg_banks = {}
        products = {}

        def aggregate(b, r):
            if not 0 <= r < OUT_BLOCKS:
                return
            for j in range(r * TILES_PER_BLOCK, (r + 1) * TILES_PER_BLOCK):
                cols = slice(j * P, (j + 1) * P)
                if b == 0:
                    agg = psum_side.tile([P, C_TILES, P], F32, tag="side")
                else:
                    agg = psum_scores.tile([P, C_TILES, P], F32, tag="scores")
                for t in range(C_TILES):
                    rows = slice(t * P, (t + 1) * P)
                    for g in range(M_PASSES):
                        nc.tensor.matmul_mx(
                            out=agg[:, t, :],
                            lhsT=v_codes[b][:, g, rows].bitcast(FP8X4),
                            lhsT_scale=v_scales[b][:, g, rows],
                            rhs=a_codes[b][:, g, cols].bitcast(FP8X4),
                            rhs_scale=a_scales[b][:, g, cols],
                            start=(g == 0),
                            stop=(g == M_PASSES - 1),
                        )
                agg_banks[(b, j)] = agg

        def residual(b, r):
            if not 0 <= r < OUT_BLOCKS:
                return
            for j in range(r * TILES_PER_BLOCK, (r + 1) * TILES_PER_BLOCK):
                residual_tile(b, j)

        def residual_tile(b, j):
            cols = slice(j * P, (j + 1) * P)
            nc.vector.scalar_tensor_tensor(
                out=y_grouped[b][:, cols, :],
                in0=agg_banks[(b, j)][:].rearrange("p t n -> p n t"),
                scalar=gain[:, 0:1],
                in1=x_sb[b][:, :, cols].rearrange("p t n -> p n t"),
                op0=ALU.mult,
                op1=ALU.add,
            )

        blocks = [(b, slice(n, n + OUT_COLS)) for b in range(IMAGES) for n in range(0, PIXELS, OUT_COLS)]
        b, cols = blocks.pop()
        middle = cols.start + OUT_COLS // 2
        blocks += [(b, slice(cols.start, middle)), (b, slice(middle, cols.stop))]

        def project(k):
            if not 0 <= k < len(blocks):
                return
            b, cols = blocks[k]
            nc.vector.quantize_mx(
                out=y_codes[b][:, cols].bitcast(FP8X4),
                scales=y_scales[b][:, cols],
                in_=y_grouped[b][:, cols, :].rearrange("p n t -> p (n t)"),
            )
            product = psum_side.tile(
                [P, D_TILES, cols.stop - cols.start], F32, tag="side", name="product"
            )
            for i in range(D_TILES):
                rows = slice(i * P, (i + 1) * P)
                nc.tensor.matmul_mx(
                    out=product[:, i, :],
                    lhsT=w_codes[:, rows].bitcast(FP8X4),
                    lhsT_scale=w_scales[:, rows],
                    rhs=y_codes[b][:, cols].bitcast(FP8X4),
                    rhs_scale=y_scales[b][:, cols],
                    start=True,
                    stop=True,
                )
            products[k] = product

        def store(k):
            if not 0 <= k < len(blocks):
                return
            b, cols = blocks[k]
            result = result_pool.tile([P, D_TILES, cols.stop - cols.start], F32, name="result")
            nc.scalar.copy(out=result[:], in_=products[k][:])
            nc.sync.dma_start(
                out=out[b].rearrange("(i p) h w -> p i (h w)", p=P)[:, :, cols], in_=result[:]
            )

        jobs = {
            0: job_v(0, 0),
            1: job_v(0, 1),
            2: (flip_w, lambda: unload_w(0), lambda: unload_w(1), pack_w),
            3: job_q(1, 0),
            4: job_q(1, 1),
            10: half_job_v(1, 0, 0),
            11: half_job_v(1, 0, 1),
            12: half_job_v(1, 1, 0),
            13: half_job_v(1, 1, 1),
        }
        REGROUP_LAG = 2
        FINISH_STEP = PIXEL_TILES + REGROUP_LAG + 3

        for h in range(HALVES):
            flip_q(0, h)
            unload_q(0, h, 0)
            unload_q(0, h, 1)
        scores(0)
        bank_maxima(0)
        negative_maximum(0)

        for s in range(ALL_KEY_TILES):
            r = s - FINISH_STEP
            following = s + 1 < ALL_KEY_TILES
            if following:
                scores(s + 1)
            if s in jobs:
                jobs[s][0]()
            aggregate(0, r)
            exponentials(s)
            column_sum(s)
            store(r - 3)
            bulk = []
            if s - 1 in jobs:
                jobs[s - 1][1]()
                bulk.append(jobs[s - 1][2])
            if s - 2 in jobs:
                bulk.append(jobs[s - 2][3])
            if 0 <= r - 1 < OUT_BLOCKS:
                bulk.append(partial(residual_tile, 0, 2 * r - 2))
                bulk.append(partial(residual_tile, 0, 2 * r - 1))
            if 0 <= r - 2 < OUT_BLOCKS:
                bulk.append(partial(project, r - 2))
            for lag in range(3):
                b, g, t = place(max(s - REGROUP_LAG - lag, 0))
                if s - REGROUP_LAG - lag >= 0 and t == PACK - 1:
                    if lag < HALVES:
                        bulk.append(partial(regroup_a, b, g, slice(lag * BANK, min((lag + 1) * BANK, SPLIT)), nc.vector.tensor_copy))
                    else:
                        bulk.append(partial(quantise_a, b, g, 0))
                        bulk.append(partial(quantise_a, b, g, 1))
            bulk = [f for f in bulk if f != nothing]
            if following:
                bank_maxima(s + 1)
            if s >= 1:
                reciprocal_sum(s - 1)
                normalise(s - 1)
            for f in bulk[:1]:
                f()
            if following:
                negative_maximum(s + 1)
            for f in bulk[1:]:
                f()

        last = ALL_KEY_TILES - 1
        r = ALL_KEY_TILES - FINISH_STEP
        reciprocal_sum(last)
        aggregate(0, r)
        store(r - 3)
        project(r - 2)
        normalise_on_both(last)
        residual(0, r - 1)
        regroup_a(1, 1, slice(0, 256), nc.vector.tensor_copy)
        regroup_a(1, 1, slice(256, 512), nc.vector.tensor_copy)
        regroup_a(1, 1, slice(512, PIXELS), nc.scalar.copy)
        store(r - 2)
        project(r - 1)
        quantise_a(1, 1, 0)
        aggregate(1, 0)
        residual(0, r)
        quantise_a(1, 1, 1)
        for d in range(OUT_BLOCKS):
            aggregate(1, d + 1)
            store(r - 1 + d)
            if d == 0:
                project(r)
            residual_tile(1, 2 * d)
            if d == OUT_BLOCKS - 1:
                project(r + d)
            residual_tile(1, 2 * d + 1)
            if 0 < d < OUT_BLOCKS - 1:
                project(r + d)
        for k in range(r - 1 + OUT_BLOCKS, len(blocks)):
            if k < len(blocks) - 1:
                project(k + 1)
            store(k)
